import numpy as np
import ml_dtypes


def mxq(x, axis, fmt="e4m3"):
    dtype, down = {"e4m3": (ml_dtypes.float8_e4m3fn, 7), "e5m2": (ml_dtypes.float8_e5m2, 14)}[fmt]
    v = np.moveaxis(np.asarray(x, np.float32).astype(ml_dtypes.bfloat16).astype(np.float64), axis, -1)
    blocks = v.reshape(v.shape[:-1] + (-1, 32))
    amax = np.abs(blocks).max(-1, keepdims=True)
    byte = np.maximum(np.where(amax > 0, np.frexp(amax)[1] - 1 + 127, 0) - down, 1)
    scale = np.exp2(byte - 127.0)
    codes = (blocks / scale).astype(np.float32).astype(dtype).astype(np.float64)
    return np.moveaxis((codes * scale).reshape(v.shape), -1, axis)


WIDE = False


def mx_kscale(k):
    if not WIDE:
        return np.ones(k)
    levels = np.array([10, -10, 5, -5, 0])
    a = np.random.permutation(np.resize(levels, k // 512 * 4)).reshape(k // 512, 4)
    idx = np.arange(k)
    return np.exp2(a[idx // 512, idx % 128 // 32])


BF16 = ml_dtypes.bfloat16


def bf(x):
    return np.asarray(x, np.float32).astype(BF16)


def f64(x):
    return np.asarray(x).astype(np.float64)


B, T, HID, H, NOPE, ROPE, VD, KV_LORA = 1, 512, 2048, 16, 64, 128, 128, 512
QK = NOPE + ROPE
HALF = ROPE // 2


def rope(x, cos, sin):
    c = cos[None, :, None, :]
    s = sin[None, :, None, :]
    x1, x2 = x[..., 0::2], x[..., 1::2]
    o1 = x1 * c - x2 * s
    o2 = x1 * s + x2 * c
    return np.stack([o1, o2], axis=-1).reshape(x.shape)


def setup_inputs():
    s = mx_kscale(HID)
    ang = np.random.uniform(-np.pi, np.pi, (T, HALF))
    return {"hidden_states": bf(np.random.standard_normal((B, T, HID)) * s),
            "rope_cos": bf(np.cos(ang)), "rope_sin": bf(np.sin(ang)),
            "Wq": bf(np.random.standard_normal((HID, H * QK)) / np.sqrt(HID) / s[:, None])}


def reference(hidden_states, rope_cos, rope_sin, Wq):
    q = (mxq(f64(hidden_states), 2, "e4m3") @ mxq(f64(Wq), 0, "e4m3")).reshape(B, T, H, QK)
    q_nope, q_rope = q[..., :NOPE], q[..., NOPE:]
    q_rope = rope(q_rope, f64(rope_cos), f64(rope_sin))
    return np.concatenate([q_nope, q_rope], axis=-1)

@@ -1,0 +1,184 @@
+from contextlib import ExitStack
+
+import concourse.mybir as mybir
+from concourse.masks import make_identity
+
+F32 = mybir.dt.float32
+BF16 = mybir.dt.bfloat16
+U32 = mybir.dt.uint32
+U8 = mybir.dt.uint8
+FP8X4 = mybir.dt.float8_e4m3fn_x4
+MULT = mybir.AluOpType.mult
+ADD = mybir.AluOpType.add
+
+P = 128
+PACK = 4
+K_PASS = P * PACK
+
+TOKENS = 512
+HIDDEN = 2048
+HEADS = 16
+NOPE = 64
+ROPE = 128
+HEAD = NOPE + ROPE
+PAIRS = ROPE // 2
+
+TOKEN_TILES = TOKENS // P
+PASSES = HIDDEN // K_PASS
+GROUP_HEADS = 4
+GROUPS = HEADS // GROUP_HEADS
+GROUP_COLS = GROUP_HEADS * HEAD
+ROPE_COLS = GROUP_HEADS * ROPE
+NOPE_COLS = GROUP_HEADS * NOPE
+
+FLOPS = 2 * TOKENS * HIDDEN * HEADS * HEAD
+
+
+def tile_multilatentattention_pb_kernel(tc, hidden_states, rope_cos, rope_sin, Wq, out):
+    nc = tc.nc
+
+    hidden_view = hidden_states.rearrange("b (p a) k -> p (b a) k", a=TOKEN_TILES)
+    cos_view = rope_cos.rearrange("(p a) i -> p a i", a=TOKEN_TILES)
+    sin_view = rope_sin.rearrange("(p a) i -> p a i", a=TOKEN_TILES)
+    out_view = out.rearrange("b (p a) h d -> p (b a) (h d)", a=TOKEN_TILES)
+    w_view = Wq.rearrange("(g p j) n -> g p j n", p=P, j=PACK)
+
+    with ExitStack() as ctx:
+        keep = ctx.enter_context(tc.tile_pool(name="keep", bufs=1))
+        grouped_pool = ctx.enter_context(tc.tile_pool(name="grouped", bufs=3))
+        codes_pool = ctx.enter_context(tc.tile_pool(name="codes", bufs=2))
+        result_pool = ctx.enter_context(tc.tile_pool(name="result", bufs=4))
+        psum_flip = ctx.enter_context(tc.psum_pool(name="psum_flip", bufs=2))
+        psum_rope = ctx.enter_context(tc.psum_pool(name="psum_rope", bufs=4))
+        psum_nope = ctx.enter_context(tc.psum_pool(name="psum_nope", bufs=2))
+
+        cos_bf = keep.tile([P, TOKEN_TILES, PAIRS], BF16, name="cos_bf")
+        sin_bf = keep.tile([P, TOKEN_TILES, PAIRS], BF16, name="sin_bf")
+        nc.scalar.dma_start(out=cos_bf[:], in_=cos_view)
+        nc.scalar.dma_start(out=sin_bf[:], in_=sin_view)
+
+        x_sb = keep.tile([P, TOKEN_TILES, HIDDEN], BF16, name="x_sb")
+        raw = {}
+
+        def load_weights(c, g):
+            raw[(c, g)] = keep.tile([P, PACK, GROUP_COLS], BF16, name="raw_%d_%d" % (c, g))
+            nc.sync.dma_start(
+                out=raw[(c, g)][:],
+                in_=w_view[g][:, :, c * GROUP_COLS : (c + 1) * GROUP_COLS],
+            )
+
+        load_weights(0, 0)
+        load_weights(0, 1)
+        nc.sync.dma_start(out=x_sb[:], in_=hidden_view)
+        for c in range(GROUPS):
+            for g in range(PASSES):
+                if (c, g) not in raw:
+                    load_weights(c, g)
+
+        first_table = keep.tile([P, TOKEN_TILES, PAIRS, 2], F32, name="first_table")
+        second_table = keep.tile([P, TOKEN_TILES, PAIRS, 2], F32, name="second_table")
+        nc.vector.tensor_copy(out=first_table[:, :, :, 0], in_=cos_bf[:])
+        nc.vector.tensor_copy(out=first_table[:, :, :, 1], in_=sin_bf[:])
+        nc.scalar.mul(out=second_table[:, :, :, 0], in_=sin_bf[:], mul=-1.0)
+        nc.scalar.copy(out=second_table[:, :, :, 1], in_=cos_bf[:])
+
+        identity = keep.tile([P, P], F32, name="identity")
+        make_identity(nc, identity[:])
+
+        x_codes = keep.tile([P, TOKEN_TILES, PASSES, P], U32, name="x_codes", align_bytes=64)
+        x_scales = keep.tile([P, TOKEN_TILES, PASSES, P], U8, name="x_scales", align_bytes=64)
+
+        def prepare_hidden(a):
+            words = x_sb[:, a, :].bitcast(F32).rearrange("p (g q u) -> p g u q", q=P, u=2)
+            x_grouped = grouped_pool.tile([P, PASSES, P, PACK], BF16, name="x_grouped", align_bytes=64)
+            x_grouped_words = x_grouped[:].bitcast(F32)
+            for half in range(2):
+                flipped = psum_flip.tile([P, 2, 2, P], F32, name="flipped")
+                for gg in range(2):
+                    for u in range(2):
+                        nc.tensor.transpose(flipped[:, gg, u, :], words[:, 2 * half + gg, u, :], identity[:])
+                nc.scalar.copy(
+                    out=x_grouped_words[:, 2 * half : 2 * half + 2],
+                    in_=flipped[:].rearrange("p g u t -> p g t u"),
+                )
+            nc.vector.quantize_mx(
+                out=x_codes[:, a].rearrange("p g t -> p (g t)").bitcast(FP8X4),
+                scales=x_scales[:, a].rearrange("p g t -> p (g t)"),
+                in_=x_grouped[:].rearrange("p g t j -> p (g t j)"),
+            )
+
+        w_codes = {}
+        w_scales = {}
+
+        def prepare_weights(c, g):
+            if g == 0:
+                w_codes[c] = codes_pool.tile([P, PASSES, GROUP_COLS], U32, name="w_codes", align_bytes=64)
+                w_scales[c] = codes_pool.tile([P, PASSES, GROUP_COLS], U8, name="w_scales", align_bytes=64)
+            by_head = raw[(c, g)][:].rearrange("p j (h x) -> p j h x", x=HEAD)
+            w_grouped = grouped_pool.tile([P, GROUP_COLS, PACK], BF16, name="w_grouped", align_bytes=64)
+            nc.scalar.copy(
+                out=w_grouped[:, 0:ROPE_COLS, :].rearrange("p (h x) j -> p h x j", h=GROUP_HEADS),
+                in_=by_head[:, :, :, NOPE:HEAD].rearrange("p j h x -> p h x j"),
+            )
+            nc.vector.tensor_copy(
+                out=w_grouped[:, ROPE_COLS:GROUP_COLS, :].rearrange("p (h c i) j -> p h c j i", h=GROUP_HEADS, i=4),
+                in_=by_head[:, :, :, 0:NOPE].rearrange("p j h (c i) -> p h c j i", i=4),
+            )
+            for first, last in ((ROPE_COLS, GROUP_COLS), (0, ROPE_COLS)):
+                nc.vector.quantize_mx(
+                    out=w_codes[c][:, g, first:last].bitcast(FP8X4),
+                    scales=w_scales[c][:, g, first:last],
+                    in_=w_grouped[:, first:last, :].rearrange("p n j -> p (n j)"),
+                )
+
+        def finish(c, a):
+            rope_ps = psum_rope.tile([P, GROUP_HEADS, PAIRS, 2], F32, name="rope_ps")
+            nope_ps = psum_nope.tile([P, GROUP_HEADS, NOPE], F32, name="nope_ps")
+            for acc, first, last in (
+                (rope_ps[:].rearrange("p h i e -> p (h i e)"), 0, ROPE_COLS),
+                (nope_ps[:].rearrange("p h x -> p (h x)"), ROPE_COLS, GROUP_COLS),
+            ):
+                for g in range(PASSES):
+                    nc.tensor.matmul_mx(
+                        out=acc,
+                        lhsT=x_codes[:, a, g, :].bitcast(FP8X4),
+                        lhsT_scale=x_scales[:, a, g, :],
+                        rhs=w_codes[c][:, g, first:last].bitcast(FP8X4),
+                        rhs_scale=w_scales[c][:, g, first:last],
+                        start=(g == 0),
+                        stop=(g == PASSES - 1),
+                    )
+            result = result_pool.tile([P, GROUP_HEADS, HEAD], F32, name="result")
+            rotated = result[:, :, NOPE:HEAD].rearrange("p h (i e) -> p h i e", e=2)
+            second_part = result_pool.tile([P, GROUP_HEADS, PAIRS, 2], F32, name="second_part")
+            shape = [P, GROUP_HEADS, PAIRS, 2]
+            nc.scalar.copy(out=result[:, :, 0:NOPE], in_=nope_ps[:])
+            nc.vector.tensor_tensor(
+                out=rotated,
+                in0=rope_ps[:, :, :, 0:1].to_broadcast(shape),
+                in1=first_table[:, a].unsqueeze(1).to_broadcast(shape),
+                op=MULT,
+            )
+            nc.vector.tensor_tensor(
+                out=second_part[:],
+                in0=rope_ps[:, :, :, 1:2].to_broadcast(shape),
+                in1=second_table[:, a].unsqueeze(1).to_broadcast(shape),
+                op=MULT,
+            )
+            nc.vector.tensor_tensor(out=rotated, in0=rotated, in1=second_part[:], op=ADD)
+            nc.sync.dma_start(
+                out=out_view[:, a, c * GROUP_COLS : (c + 1) * GROUP_COLS],
+                in_=result[:].rearrange("p h d -> p (h d)"),
+            )
+
+        prepare_weights(0, 0)
+        prepare_weights(0, 1)
+        for a in range(TOKEN_TILES):
+            prepare_hidden(a)
+        prepare_weights(0, 2)
+        prepare_weights(0, 3)
+        for c in range(GROUPS):
+            for step in range(TOKEN_TILES):
+                if c + 1 < GROUPS:
+                    prepare_weights(c + 1, step)
+                finish(c, step)

@@ -28,10 +28,14 @@ PASSES = HIDDEN // K_PASS
 GROUP_HEADS = 4
 GROUPS = HEADS // GROUP_HEADS
 GROUP_COLS = GROUP_HEADS * HEAD
-ROPE_COLS = GROUP_HEADS * ROPE
-NOPE_COLS = GROUP_HEADS * NOPE
+WIDTH = {"rope": ROPE, "nope": NOPE}
+FIRST = {"rope": NOPE, "nope": 0}
 
 FLOPS = 2 * TOKENS * HIDDEN * HEADS * HEAD
+
+BLOCKS_AHEAD = 10
+STEPS = (GROUPS + 1) * PASSES
+VECTOR_NOPE_HEADS = 2
 
 
 def tile_multilatentattention_pb_kernel(tc, hidden_states, rope_cos, rope_sin, Wq, out):
@@ -45,35 +49,41 @@ def tile_multilatentattention_pb_kernel(tc, hidden_states, rope_cos, rope_sin, W
 
     with ExitStack() as ctx:
         keep = ctx.enter_context(tc.tile_pool(name="keep", bufs=1))
-        grouped_pool = ctx.enter_context(tc.tile_pool(name="grouped", bufs=3))
+        grouped_pool = ctx.enter_context(tc.tile_pool(name="grouped", bufs=4))
         codes_pool = ctx.enter_context(tc.tile_pool(name="codes", bufs=2))
-        result_pool = ctx.enter_context(tc.tile_pool(name="result", bufs=4))
-        psum_flip = ctx.enter_context(tc.psum_pool(name="psum_flip", bufs=2))
-        psum_rope = ctx.enter_context(tc.psum_pool(name="psum_rope", bufs=4))
-        psum_nope = ctx.enter_context(tc.psum_pool(name="psum_nope", bufs=2))
+        result_pool = ctx.enter_context(tc.tile_pool(name="result", bufs=6))
+        psum_rope = ctx.enter_context(tc.psum_pool(name="psum_rope", bufs=2))
+        psum_small = ctx.enter_context(tc.psum_pool(name="psum_small", bufs=4))
+        ctx.enter_context(tc.manual_schedule())
 
         cos_bf = keep.tile([P, TOKEN_TILES, PAIRS], BF16, name="cos_bf")
         sin_bf = keep.tile([P, TOKEN_TILES, PAIRS], BF16, name="sin_bf")
         nc.scalar.dma_start(out=cos_bf[:], in_=cos_view)
         nc.scalar.dma_start(out=sin_bf[:], in_=sin_view)
 
-        x_sb = keep.tile([P, TOKEN_TILES, HIDDEN], BF16, name="x_sb")
+        x_sb = {}
         raw = {}
 
-        def load_weights(c, g):
-            raw[(c, g)] = keep.tile([P, PACK, GROUP_COLS], BF16, name="raw_%d_%d" % (c, g))
-            nc.sync.dma_start(
-                out=raw[(c, g)][:],
-                in_=w_view[g][:, :, c * GROUP_COLS : (c + 1) * GROUP_COLS],
-            )
+        def load(kind, c, g):
+            if kind == "x":
+                x_sb[c] = keep.tile([P, HIDDEN], BF16, name="x_sb_%d" % c)
+                nc.sync.dma_start(out=x_sb[c][:], in_=hidden_view[:, c, :])
+            else:
+                raw[(c, g)] = keep.tile([P, PACK, GROUP_COLS], BF16, name="raw_%d_%d" % (c, g))
+                nc.sync.dma_start(
+                    out=raw[(c, g)][:],
+                    in_=w_view[g][:, :, c * GROUP_COLS : (c + 1) * GROUP_COLS],
+                )
 
-        load_weights(0, 0)
-        load_weights(0, 1)
-        nc.sync.dma_start(out=x_sb[:], in_=hidden_view)
-        for c in range(GROUPS):
+        loads = []
+        for g in range(PASSES):
+            loads.append(("w", 0, g))
+            loads.append(("x", g, 0))
+        for c in range(1, GROUPS):
             for g in range(PASSES):
-                if (c, g) not in raw:
-                    load_weights(c, g)
+                loads.append(("w", c, g))
+        for kind, c, g in loads[0:BLOCKS_AHEAD]:
+            load(kind, c, g)
 
         first_table = keep.tile([P, TOKEN_TILES, PAIRS, 2], F32, name="first_table")
         second_table = keep.tile([P, TOKEN_TILES, PAIRS, 2], F32, name="second_table")
@@ -87,13 +97,14 @@ def tile_multilatentattention_pb_kernel(tc, hidden_states, rope_cos, rope_sin, W
 
         x_codes = keep.tile([P, TOKEN_TILES, PASSES, P], U32, name="x_codes", align_bytes=64)
         x_scales = keep.tile([P, TOKEN_TILES, PASSES, P], U8, name="x_scales", align_bytes=64)
+        x_grouped = {}
 
-        def prepare_hidden(a):
-            words = x_sb[:, a, :].bitcast(F32).rearrange("p (g q u) -> p g u q", q=P, u=2)
-            x_grouped = grouped_pool.tile([P, PASSES, P, PACK], BF16, name="x_grouped", align_bytes=64)
-            x_grouped_words = x_grouped[:].bitcast(F32)
+        def flip_hidden(a):
+            words = x_sb[a][:].bitcast(F32).rearrange("p (g q u) -> p g u q", q=P, u=2)
+            x_grouped[a] = grouped_pool.tile([P, PASSES, P, PACK], BF16, name="x_grouped", align_bytes=64)
+            x_grouped_words = x_grouped[a][:].bitcast(F32)
             for half in range(2):
-                flipped = psum_flip.tile([P, 2, 2, P], F32, name="flipped")
+                flipped = psum_small.tile([P, 2, 2, P], F32, name="small_ps")
                 for gg in range(2):
                     for u in range(2):
                         nc.tensor.transpose(flipped[:, gg, u, :], words[:, 2 * half + gg, u, :], identity[:])
@@ -101,84 +112,140 @@ def tile_multilatentattention_pb_kernel(tc, hidden_states, rope_cos, rope_sin, W
                     out=x_grouped_words[:, 2 * half : 2 * half + 2],
                     in_=flipped[:].rearrange("p g u t -> p g t u"),
                 )
+
+        def quantize_hidden(a):
             nc.vector.quantize_mx(
                 out=x_codes[:, a].rearrange("p g t -> p (g t)").bitcast(FP8X4),
                 scales=x_scales[:, a].rearrange("p g t -> p (g t)"),
-                in_=x_grouped[:].rearrange("p g t j -> p (g t j)"),
+                in_=x_grouped[a][:].rearrange("p g t j -> p (g t j)"),
             )
 
+        w_grouped = {}
         w_codes = {}
         w_scales = {}
 
-        def prepare_weights(c, g):
-            if g == 0:
-                w_codes[c] = codes_pool.tile([P, PASSES, GROUP_COLS], U32, name="w_codes", align_bytes=64)
-                w_scales[c] = codes_pool.tile([P, PASSES, GROUP_COLS], U8, name="w_scales", align_bytes=64)
+        def interleave(engine, part, c, g, h0, h1):
+            if (part, c, g) not in w_grouped:
+                w_grouped[(part, c, g)] = grouped_pool.tile(
+                    [P, GROUP_HEADS * WIDTH[part], PACK], BF16, name=part + "_grouped", align_bytes=64
+                )
             by_head = raw[(c, g)][:].rearrange("p j (h x) -> p j h x", x=HEAD)
-            w_grouped = grouped_pool.tile([P, GROUP_COLS, PACK], BF16, name="w_grouped", align_bytes=64)
-            nc.scalar.copy(
-                out=w_grouped[:, 0:ROPE_COLS, :].rearrange("p (h x) j -> p h x j", h=GROUP_HEADS),
-                in_=by_head[:, :, :, NOPE:HEAD].rearrange("p j h x -> p h x j"),
-            )
-            nc.vector.tensor_copy(
-                out=w_grouped[:, ROPE_COLS:GROUP_COLS, :].rearrange("p (h c i) j -> p h c j i", h=GROUP_HEADS, i=4),
-                in_=by_head[:, :, :, 0:NOPE].rearrange("p j h (c i) -> p h c j i", i=4),
-            )
-            for first, last in ((ROPE_COLS, GROUP_COLS), (0, ROPE_COLS)):
-                nc.vector.quantize_mx(
-                    out=w_codes[c][:, g, first:last].bitcast(FP8X4),
-                    scales=w_scales[c][:, g, first:last],
-                    in_=w_grouped[:, first:last, :].rearrange("p n j -> p (n j)"),
+            source = by_head[:, :, h0:h1, FIRST[part] : FIRST[part] + WIDTH[part]]
+            target = w_grouped[(part, c, g)][:, h0 * WIDTH[part] : h1 * WIDTH[part], :]
+            if engine == "scalar":
+                nc.scalar.copy(
+                    out=target.rearrange("p (h x) j -> p h x j", h=h1 - h0),
+                    in_=source.rearrange("p j h x -> p h x j"),
+                )
+            else:
+                nc.vector.tensor_copy(
+                    out=target.rearrange("p (h c i) j -> p h c j i", h=h1 - h0, i=4),
+                    in_=source.rearrange("p j h (c i) -> p h c j i", i=4),
                 )
 
-        def finish(c, a):
-            rope_ps = psum_rope.tile([P, GROUP_HEADS, PAIRS, 2], F32, name="rope_ps")
-            nope_ps = psum_nope.tile([P, GROUP_HEADS, NOPE], F32, name="nope_ps")
-            for acc, first, last in (
-                (rope_ps[:].rearrange("p h i e -> p (h i e)"), 0, ROPE_COLS),
-                (nope_ps[:].rearrange("p h x -> p (h x)"), ROPE_COLS, GROUP_COLS),
-            ):
-                for g in range(PASSES):
-                    nc.tensor.matmul_mx(
-                        out=acc,
-                        lhsT=x_codes[:, a, g, :].bitcast(FP8X4),
-                        lhsT_scale=x_scales[:, a, g, :],
-                        rhs=w_codes[c][:, g, first:last].bitcast(FP8X4),
-                        rhs_scale=w_scales[c][:, g, first:last],
-                        start=(g == 0),
-                        stop=(g == PASSES - 1),
-                    )
-            result = result_pool.tile([P, GROUP_HEADS, HEAD], F32, name="result")
-            rotated = result[:, :, NOPE:HEAD].rearrange("p h (i e) -> p h i e", e=2)
-            second_part = result_pool.tile([P, GROUP_HEADS, PAIRS, 2], F32, name="second_part")
-            shape = [P, GROUP_HEADS, PAIRS, 2]
-            nc.scalar.copy(out=result[:, :, 0:NOPE], in_=nope_ps[:])
+        def quantize(part, c, g):
+            if g == 0:
+                columns = GROUP_HEADS * WIDTH[part]
+                w_codes[(part, c)] = codes_pool.tile([P, PASSES, columns], U32, name=part + "_codes", align_bytes=64)
+                w_scales[(part, c)] = codes_pool.tile([P, PASSES, columns], U8, name=part + "_scales", align_bytes=64)
+            nc.vector.quantize_mx(
+                out=w_codes[(part, c)][:, g, :].bitcast(FP8X4),
+                scales=w_scales[(part, c)][:, g, :],
+                in_=w_grouped[(part, c, g)][:].rearrange("p n j -> p (n j)"),
+            )
+
+        sums = {}
+        result = {}
+        second_part = {}
+        shape = [P, GROUP_HEADS, PAIRS, 2]
+
+        def multiply(part, c, a):
+            if part == "rope":
+                sums[(part, c, a)] = psum_rope.tile(shape, F32, name="rope_ps")
+                acc = sums[(part, c, a)][:].rearrange("p h i e -> p (h i e)")
+            else:
+                sums[(part, c, a)] = psum_small.tile([P, GROUP_HEADS, NOPE], F32, name="small_ps")
+                acc = sums[(part, c, a)][:].rearrange("p h x -> p (h x)")
+            for g in range(PASSES):
+                nc.tensor.matmul_mx(
+                    out=acc,
+                    lhsT=x_codes[:, a, g, :].bitcast(FP8X4),
+                    lhsT_scale=x_scales[:, a, g, :],
+                    rhs=w_codes[(part, c)][:, g, :].bitcast(FP8X4),
+                    rhs_scale=w_scales[(part, c)][:, g, :],
+                    start=(g == 0),
+                    stop=(g == PASSES - 1),
+                )
+
+        def rotated(c, a):
+            return result[(c, a)][:, :, NOPE:HEAD].rearrange("p h (i e) -> p h i e", e=2)
+
+        def first_product(c, a):
+            result[(c, a)] = result_pool.tile([P, GROUP_HEADS, HEAD], F32, name="result")
             nc.vector.tensor_tensor(
-                out=rotated,
-                in0=rope_ps[:, :, :, 0:1].to_broadcast(shape),
+                out=rotated(c, a),
+                in0=sums[("rope", c, a)][:, :, :, 0:1].to_broadcast(shape),
                 in1=first_table[:, a].unsqueeze(1).to_broadcast(shape),
                 op=MULT,
             )
+
+        def second_product(c, a):
+            second_part[(c, a)] = result_pool.tile(shape, F32, name="second_part")
             nc.vector.tensor_tensor(
-                out=second_part[:],
-                in0=rope_ps[:, :, :, 1:2].to_broadcast(shape),
+                out=second_part[(c, a)][:],
+                in0=sums[("rope", c, a)][:, :, :, 1:2].to_broadcast(shape),
                 in1=second_table[:, a].unsqueeze(1).to_broadcast(shape),
                 op=MULT,
             )
-            nc.vector.tensor_tensor(out=rotated, in0=rotated, in1=second_part[:], op=ADD)
+
+        def add_products(c, a):
+            nc.vector.tensor_tensor(out=rotated(c, a), in0=rotated(c, a), in1=second_part[(c, a)][:], op=ADD)
+
+        def finish(c, a):
+            nc.scalar.copy(out=result[(c, a)][:, :, 0:NOPE], in_=sums[("nope", c, a)][:])
             nc.sync.dma_start(
                 out=out_view[:, a, c * GROUP_COLS : (c + 1) * GROUP_COLS],
-                in_=result[:].rearrange("p h d -> p (h d)"),
+                in_=result[(c, a)][:].rearrange("p h d -> p (h d)"),
             )
 
-        prepare_weights(0, 0)
-        prepare_weights(0, 1)
-        for a in range(TOKEN_TILES):
-            prepare_hidden(a)
-        prepare_weights(0, 2)
-        prepare_weights(0, 3)
-        for c in range(GROUPS):
-            for step in range(TOKEN_TILES):
-                if c + 1 < GROUPS:
-                    prepare_weights(c + 1, step)
-                finish(c, step)
+        def scalar_share(s):
+            c, g = s // PASSES, s % PASSES
+            if c == 0:
+                interleave("scalar", "rope", c, g, 0, 2)
+            elif c < GROUPS:
+                interleave("scalar", "rope", c, g, 0, GROUP_HEADS)
+                interleave("scalar", "nope", c, g, VECTOR_NOPE_HEADS, GROUP_HEADS)
+
+        scalar_share(0)
+        for s in range(STEPS):
+            c, g = s // PASSES, s % PASSES
+            for kind, lc, lg in loads[BLOCKS_AHEAD + s : BLOCKS_AHEAD + s + 1]:
+                load(kind, lc, lg)
+            if c == 0:
+                flip_hidden(g)
+            if s > PASSES:
+                finish((s - 1) // PASSES - 1, (s - 1) % PASSES)
+            scalar_share(s + 1)
+            if c == 0:
+                interleave("vector", "rope", c, g, 2, GROUP_HEADS)
+                interleave("vector", "nope", c, g, 0, GROUP_HEADS)
+            elif c < GROUPS:
+                interleave("vector", "nope", c, g, 0, VECTOR_NOPE_HEADS)
+            if c > 0:
+                first_product(c - 1, g)
+            if c == 0 and g > 0:
+                quantize_hidden(g - 1)
+            if c < GROUPS:
+                quantize("rope", c, g)
+            if c > 0:
+                second_product(c - 1, g)
+            if c < GROUPS:
+                quantize("nope", c, g)
+            if s == PASSES - 1:
+                quantize_hidden(g)
+            if c > 0:
+                add_products(c - 1, g)
+            if PASSES - 1 <= s < STEPS - 1:
+                multiply("rope", (s + 1) // PASSES - 1, (s + 1) % PASSES)
+                multiply("nope", (s + 1) // PASSES - 1, (s + 1) % PASSES)
+        finish(GROUPS - 1, PASSES - 1)

@@ -134,8 +134,8 @@ def tile_multilatentattention_pb_kernel(tc, hidden_states, rope_cos, rope_sin, W
             target = w_grouped[(part, c, g)][:, h0 * WIDTH[part] : h1 * WIDTH[part], :]
             if engine == "scalar":
                 nc.scalar.copy(
-                    out=target.rearrange("p (h x) j -> p h x j", h=h1 - h0),
-                    in_=source.rearrange("p j h x -> p h x j"),
+                    out=target.rearrange("p (h c i) j -> p h c j i", h=h1 - h0, i=4),
+                    in_=source.rearrange("p j h (c i) -> p h c j i", i=4),
                 )
             else:
                 nc.vector.tensor_copy(

@@ -51,8 +51,8 @@ def tile_multilatentattention_pb_kernel(tc, hidden_states, rope_cos, rope_sin, W
         keep = ctx.enter_context(tc.tile_pool(name="keep", bufs=1))
         grouped_pool = ctx.enter_context(tc.tile_pool(name="grouped", bufs=4))
         codes_pool = ctx.enter_context(tc.tile_pool(name="codes", bufs=2))
-        result_pool = ctx.enter_context(tc.tile_pool(name="result", bufs=6))
-        psum_rope = ctx.enter_context(tc.psum_pool(name="psum_rope", bufs=2))
+        result_pool = ctx.enter_context(tc.tile_pool(name="result", bufs=8))
+        psum_rope = ctx.enter_context(tc.psum_pool(name="psum_rope", bufs=3))
         psum_small = ctx.enter_context(tc.psum_pool(name="psum_small", bufs=4))
         ctx.enter_context(tc.manual_schedule())
 
@@ -177,11 +177,15 @@ def tile_multilatentattention_pb_kernel(tc, hidden_states, rope_cos, rope_sin, W
                     stop=(g == PASSES - 1),
                 )
 
+        def new_result(c, a):
+            if (c, a) not in result:
+                result[(c, a)] = result_pool.tile([P, GROUP_HEADS, HEAD], F32, name="result")
+
         def rotated(c, a):
             return result[(c, a)][:, :, NOPE:HEAD].rearrange("p h (i e) -> p h i e", e=2)
 
         def first_product(c, a):
-            result[(c, a)] = result_pool.tile([P, GROUP_HEADS, HEAD], F32, name="result")
+            new_result(c, a)
             nc.vector.tensor_tensor(
                 out=rotated(c, a),
                 in0=sums[("rope", c, a)][:, :, :, 0:1].to_broadcast(shape),
@@ -190,7 +194,7 @@ def tile_multilatentattention_pb_kernel(tc, hidden_states, rope_cos, rope_sin, W
             )
 
         def second_product(c, a):
-            second_part[(c, a)] = result_pool.tile(shape, F32, name="second_part")
+            second_part[(c, a)] = result_pool.tile(shape, F32, name="second_part", bufs=3)
             nc.vector.tensor_tensor(
                 out=second_part[(c, a)][:],
                 in0=sums[("rope", c, a)][:, :, :, 1:2].to_broadcast(shape),
@@ -199,53 +203,79 @@ def tile_multilatentattention_pb_kernel(tc, hidden_states, rope_cos, rope_sin, W
             )
 
         def add_products(c, a):
-            nc.vector.tensor_tensor(out=rotated(c, a), in0=rotated(c, a), in1=second_part[(c, a)][:], op=ADD)
+            engine = nc.gpsimd if (c == GROUPS - 1 and a < PASSES - 1) else nc.vector
+            engine.tensor_tensor(out=rotated(c, a), in0=rotated(c, a), in1=second_part[(c, a)][:], op=ADD)
 
-        def finish(c, a):
+        def copy_unchanged(c, a):
+            new_result(c, a)
             nc.scalar.copy(out=result[(c, a)][:, :, 0:NOPE], in_=sums[("nope", c, a)][:])
+
+        def store(c, a):
             nc.sync.dma_start(
                 out=out_view[:, a, c * GROUP_COLS : (c + 1) * GROUP_COLS],
                 in_=result[(c, a)][:].rearrange("p h d -> p (h d)"),
             )
 
+        LAST = GROUPS - 1
+        prepare = {}
+        for s in range(GROUPS * PASSES):
+            prepare[s] = [("rope", s // PASSES, s % PASSES)]
+            if s // PASSES < LAST:
+                prepare[s].append(("nope", s // PASSES, s % PASSES))
+        for g in range(PASSES):
+            prepare[LAST * PASSES + g // 2].append(("nope", LAST, g))
+
         def scalar_share(s):
-            c, g = s // PASSES, s % PASSES
-            if c == 0:
-                interleave("scalar", "rope", c, g, 0, 2)
-            elif c < GROUPS:
-                interleave("scalar", "rope", c, g, 0, GROUP_HEADS)
-                interleave("scalar", "nope", c, g, VECTOR_NOPE_HEADS, GROUP_HEADS)
+            for part, c, g in prepare.get(s, []):
+                if part == "rope":
+                    interleave("scalar", part, c, g, 0, 2 if c == 0 else GROUP_HEADS)
+                elif c > 0:
+                    interleave("scalar", part, c, g, VECTOR_NOPE_HEADS, GROUP_HEADS)
+
+        def vector_share(s):
+            for part, c, g in prepare.get(s, []):
+                if part == "nope":
+                    interleave("vector", part, c, g, 0, GROUP_HEADS if c == 0 else VECTOR_NOPE_HEADS)
+                elif c == 0:
+                    interleave("vector", part, c, g, 2, GROUP_HEADS)
+
+        def rotation(s):
+            return s // PASSES - 1, s % PASSES
 
         scalar_share(0)
         for s in range(STEPS):
-            c, g = s // PASSES, s % PASSES
             for kind, lc, lg in loads[BLOCKS_AHEAD + s : BLOCKS_AHEAD + s + 1]:
                 load(kind, lc, lg)
-            if c == 0:
-                flip_hidden(g)
+            if s < PASSES:
+                flip_hidden(s)
             if s > PASSES:
-                finish((s - 1) // PASSES - 1, (s - 1) % PASSES)
+                if rotation(s - 1)[0] < LAST:
+                    copy_unchanged(rotation(s - 1)[0], rotation(s - 1)[1])
+                store(rotation(s - 1)[0], rotation(s - 1)[1])
+            if LAST * PASSES + 3 <= s < STEPS - 1:
+                copy_unchanged(LAST, s - LAST * PASSES - 3)
             scalar_share(s + 1)
-            if c == 0:
-                interleave("vector", "rope", c, g, 2, GROUP_HEADS)
-                interleave("vector", "nope", c, g, 0, GROUP_HEADS)
-            elif c < GROUPS:
-                interleave("vector", "nope", c, g, 0, VECTOR_NOPE_HEADS)
-            if c > 0:
-                first_product(c - 1, g)
-            if c == 0 and g > 0:
-                quantize_hidden(g - 1)
-            if c < GROUPS:
-                quantize("rope", c, g)
-            if c > 0:
-                second_product(c - 1, g)
-            if c < GROUPS:
-                quantize("nope", c, g)
+            vector_share(s)
+            units = list(prepare.get(s, []))
+            if s >= PASSES:
+                first_product(rotation(s)[0], rotation(s)[1])
+            if 0 < s < PASSES:
+                quantize_hidden(s - 1)
+            if len(units) > 1 or s < PASSES:
+                quantize(units[0][0], units[0][1], units[0][2])
+                units = units[1:]
+            if s >= PASSES:
+                second_product(rotation(s)[0], rotation(s)[1])
+            for part, c, g in units:
+                quantize(part, c, g)
             if s == PASSES - 1:
-                quantize_hidden(g)
-            if c > 0:
-                add_products(c - 1, g)
+                quantize_hidden(s)
+            if s >= PASSES:
+                add_products(rotation(s)[0], rotation(s)[1])
             if PASSES - 1 <= s < STEPS - 1:
-                multiply("rope", (s + 1) // PASSES - 1, (s + 1) % PASSES)
-                multiply("nope", (s + 1) // PASSES - 1, (s + 1) % PASSES)
-        finish(GROUPS - 1, PASSES - 1)
+                multiply("rope", rotation(s + 1)[0], rotation(s + 1)[1])
+                if rotation(s + 1)[0] < LAST:
+                    multiply("nope", rotation(s + 1)[0], rotation(s + 1)[1])
+            if LAST * PASSES + 1 <= s < LAST * PASSES + 1 + PASSES:
+                multiply("nope", LAST, s - LAST * PASSES - 1)
+        store(LAST, PASSES - 1)

@@ -203,12 +203,18 @@ def tile_multilatentattention_pb_kernel(tc, hidden_states, rope_cos, rope_sin, W
             )
 
         def add_products(c, a):
-            engine = nc.gpsimd if (c == GROUPS - 1 and a < PASSES - 1) else nc.vector
+            engine = nc.vector if (c == GROUPS - 1 and a == PASSES - 1) else nc.gpsimd
             engine.tensor_tensor(out=rotated(c, a), in0=rotated(c, a), in1=second_part[(c, a)][:], op=ADD)
 
-        def copy_unchanged(c, a):
+        def copy_unchanged(engine, c, a):
             new_result(c, a)
-            nc.scalar.copy(out=result[(c, a)][:, :, 0:NOPE], in_=sums[("nope", c, a)][:])
+            copy = nc.scalar.copy if engine == "scalar" else nc.vector.tensor_copy
+            copy(out=result[(c, a)][:, :, 0:NOPE], in_=sums[("nope", c, a)][:])
+
+        gate_word = keep.tile([P, 1], U32, name="gate_word")
+
+        def wait_for_codes(c, g):
+            nc.gpsimd.tensor_copy(out=gate_word[:], in_=w_codes[("rope", c)][:, g, 0:1])
 
         def store(c, a):
             nc.sync.dma_start(
@@ -248,34 +254,32 @@ def tile_multilatentattention_pb_kernel(tc, hidden_states, rope_cos, rope_sin, W
                 load(kind, lc, lg)
             if s < PASSES:
                 flip_hidden(s)
-            if s > PASSES:
-                if rotation(s - 1)[0] < LAST:
-                    copy_unchanged(rotation(s - 1)[0], rotation(s - 1)[1])
-                store(rotation(s - 1)[0], rotation(s - 1)[1])
             if LAST * PASSES + 3 <= s < STEPS - 1:
-                copy_unchanged(LAST, s - LAST * PASSES - 3)
+                copy_unchanged("scalar", LAST, s - LAST * PASSES - 3)
             scalar_share(s + 1)
             vector_share(s)
-            units = list(prepare.get(s, []))
-            if s >= PASSES:
-                first_product(rotation(s)[0], rotation(s)[1])
             if 0 < s < PASSES:
                 quantize_hidden(s - 1)
-            if len(units) > 1 or s < PASSES:
-                quantize(units[0][0], units[0][1], units[0][2])
-                units = units[1:]
-            if s >= PASSES:
-                second_product(rotation(s)[0], rotation(s)[1])
-            for part, c, g in units:
+            for part, c, g in prepare.get(s, []):
                 quantize(part, c, g)
             if s == PASSES - 1:
                 quantize_hidden(s)
+            if s > PASSES:
+                if s < GROUPS * PASSES:
+                    wait_for_codes(s // PASSES, s % PASSES)
+                add_products(rotation(s - 1)[0], rotation(s - 1)[1])
             if s >= PASSES:
-                add_products(rotation(s)[0], rotation(s)[1])
+                first_product(rotation(s)[0], rotation(s)[1])
+                second_product(rotation(s)[0], rotation(s)[1])
+            if s > PASSES:
+                if rotation(s - 1)[0] < LAST:
+                    copy_unchanged("vector", rotation(s - 1)[0], rotation(s - 1)[1])
+                store(rotation(s - 1)[0], rotation(s - 1)[1])
             if PASSES - 1 <= s < STEPS - 1:
                 multiply("rope", rotation(s + 1)[0], rotation(s + 1)[1])
                 if rotation(s + 1)[0] < LAST:
                     multiply("nope", rotation(s + 1)[0], rotation(s + 1)[1])
             if LAST * PASSES + 1 <= s < LAST * PASSES + 1 + PASSES:
                 multiply("nope", LAST, s - LAST * PASSES - 1)
+        add_products(LAST, PASSES - 1)
         store(LAST, PASSES - 1)

@@ -35,7 +35,8 @@ FLOPS = 2 * TOKENS * HIDDEN * HEADS * HEAD
 
 BLOCKS_AHEAD = 10
 STEPS = (GROUPS + 1) * PASSES
-VECTOR_NOPE_HEADS = 2
+HIDDEN_STEP = (3, 4, 5, 6)
+VECTOR_NOPE_COLUMNS = 48
 
 
 def tile_multilatentattention_pb_kernel(tc, hidden_states, rope_cos, rope_sin, Wq, out):
@@ -52,14 +53,14 @@ def tile_multilatentattention_pb_kernel(tc, hidden_states, rope_cos, rope_sin, W
         grouped_pool = ctx.enter_context(tc.tile_pool(name="grouped", bufs=4))
         codes_pool = ctx.enter_context(tc.tile_pool(name="codes", bufs=2))
         result_pool = ctx.enter_context(tc.tile_pool(name="result", bufs=8))
-        psum_rope = ctx.enter_context(tc.psum_pool(name="psum_rope", bufs=3))
+        psum_rope = ctx.enter_context(tc.psum_pool(name="psum_rope", bufs=4))
         psum_small = ctx.enter_context(tc.psum_pool(name="psum_small", bufs=4))
         ctx.enter_context(tc.manual_schedule())
 
         cos_bf = keep.tile([P, TOKEN_TILES, PAIRS], BF16, name="cos_bf")
         sin_bf = keep.tile([P, TOKEN_TILES, PAIRS], BF16, name="sin_bf")
-        nc.scalar.dma_start(out=cos_bf[:], in_=cos_view)
-        nc.scalar.dma_start(out=sin_bf[:], in_=sin_view)
+        nc.sync.dma_start(out=cos_bf[:], in_=cos_view)
+        nc.sync.dma_start(out=sin_bf[:], in_=sin_view)
 
         x_sb = {}
         raw = {}
@@ -76,12 +77,11 @@ def tile_multilatentattention_pb_kernel(tc, hidden_states, rope_cos, rope_sin, W
                 )
 
         loads = []
-        for g in range(PASSES):
-            loads.append(("w", 0, g))
-            loads.append(("x", g, 0))
-        for c in range(1, GROUPS):
-            for g in range(PASSES):
-                loads.append(("w", c, g))
+        for s in range(GROUPS * PASSES):
+            loads.append(("w", s // PASSES, s % PASSES))
+            for a in range(TOKEN_TILES):
+                if HIDDEN_STEP[a] - 1 == s:
+                    loads.append(("x", a, 0))
         for kind, c, g in loads[0:BLOCKS_AHEAD]:
             load(kind, c, g)
 
@@ -104,7 +104,7 @@ def tile_multilatentattention_pb_kernel(tc, hidden_states, rope_cos, rope_sin, W
             x_grouped[a] = grouped_pool.tile([P, PASSES, P, PACK], BF16, name="x_grouped", align_bytes=64)
             x_grouped_words = x_grouped[a][:].bitcast(F32)
             for half in range(2):
-                flipped = psum_small.tile([P, 2, 2, P], F32, name="small_ps")
+                flipped = psum_rope.tile([P, 2, 2, P], F32, name="rope_ps")
                 for gg in range(2):
                     for u in range(2):
                         nc.tensor.transpose(flipped[:, gg, u, :], words[:, 2 * half + gg, u, :], identity[:])
@@ -124,24 +124,19 @@ def tile_multilatentattention_pb_kernel(tc, hidden_states, rope_cos, rope_sin, W
         w_codes = {}
         w_scales = {}
 
-        def interleave(engine, part, c, g, h0, h1):
+        def interleave(engine, part, c, g, h0, h1, x0, x1):
             if (part, c, g) not in w_grouped:
                 w_grouped[(part, c, g)] = grouped_pool.tile(
                     [P, GROUP_HEADS * WIDTH[part], PACK], BF16, name=part + "_grouped", align_bytes=64
                 )
             by_head = raw[(c, g)][:].rearrange("p j (h x) -> p j h x", x=HEAD)
-            source = by_head[:, :, h0:h1, FIRST[part] : FIRST[part] + WIDTH[part]]
-            target = w_grouped[(part, c, g)][:, h0 * WIDTH[part] : h1 * WIDTH[part], :]
-            if engine == "scalar":
-                nc.scalar.copy(
-                    out=target.rearrange("p (h c i) j -> p h c j i", h=h1 - h0, i=4),
-                    in_=source.rearrange("p j h (c i) -> p h c j i", i=4),
-                )
-            else:
-                nc.vector.tensor_copy(
-                    out=target.rearrange("p (h c i) j -> p h c j i", h=h1 - h0, i=4),
-                    in_=source.rearrange("p j h (c i) -> p h c j i", i=4),
-                )
+            source = by_head[:, :, h0:h1, FIRST[part] + x0 : FIRST[part] + x1]
+            target = w_grouped[(part, c, g)][:].rearrange("p (h x) j -> p h x j", h=GROUP_HEADS)[:, h0:h1, x0:x1, :]
+            copy = nc.scalar.copy if engine == "scalar" else nc.vector.tensor_copy
+            copy(
+                out=target.rearrange("p h (c i) j -> p h c j i", i=4),
+                in_=source.rearrange("p j h (c i) -> p h c j i", i=4),
+            )
 
         def quantize(part, c, g):
             if g == 0:
@@ -234,16 +229,16 @@ def tile_multilatentattention_pb_kernel(tc, hidden_states, rope_cos, rope_sin, W
         def scalar_share(s):
             for part, c, g in prepare.get(s, []):
                 if part == "rope":
-                    interleave("scalar", part, c, g, 0, 2 if c == 0 else GROUP_HEADS)
+                    interleave("scalar", part, c, g, 0, 2 if c == 0 else GROUP_HEADS, 0, ROPE)
                 elif c > 0:
-                    interleave("scalar", part, c, g, VECTOR_NOPE_HEADS, GROUP_HEADS)
+                    interleave("scalar", part, c, g, 0, GROUP_HEADS, VECTOR_NOPE_COLUMNS, NOPE)
 
         def vector_share(s):
             for part, c, g in prepare.get(s, []):
                 if part == "nope":
-                    interleave("vector", part, c, g, 0, GROUP_HEADS if c == 0 else VECTOR_NOPE_HEADS)
+                    interleave("vector", part, c, g, 0, GROUP_HEADS, 0, NOPE if c == 0 else VECTOR_NOPE_COLUMNS)
                 elif c == 0:
-                    interleave("vector", part, c, g, 2, GROUP_HEADS)
+                    interleave("vector", part, c, g, 2, GROUP_HEADS, 0, ROPE)
 
         def rotation(s):
             return s // PASSES - 1, s % PASSES
@@ -252,18 +247,14 @@ def tile_multilatentattention_pb_kernel(tc, hidden_states, rope_cos, rope_sin, W
         for s in range(STEPS):
             for kind, lc, lg in loads[BLOCKS_AHEAD + s : BLOCKS_AHEAD + s + 1]:
                 load(kind, lc, lg)
-            if s < PASSES:
-                flip_hidden(s)
             if LAST * PASSES + 3 <= s < STEPS - 1:
                 copy_unchanged("scalar", LAST, s - LAST * PASSES - 3)
             scalar_share(s + 1)
             vector_share(s)
-            if 0 < s < PASSES:
-                quantize_hidden(s - 1)
+            if s in HIDDEN_STEP:
+                quantize_hidden(HIDDEN_STEP.index(s))
             for part, c, g in prepare.get(s, []):
                 quantize(part, c, g)
-            if s == PASSES - 1:
-                quantize_hidden(s)
             if s > PASSES:
                 if s < GROUPS * PASSES:
                     wait_for_codes(s // PASSES, s % PASSES)
@@ -281,5 +272,7 @@ def tile_multilatentattention_pb_kernel(tc, hidden_states, rope_cos, rope_sin, W
                     multiply("nope", rotation(s + 1)[0], rotation(s + 1)[1])
             if LAST * PASSES + 1 <= s < LAST * PASSES + 1 + PASSES:
                 multiply("nope", LAST, s - LAST * PASSES - 1)
+            if s + 2 in HIDDEN_STEP:
+                flip_hidden(HIDDEN_STEP.index(s + 2))
         add_products(LAST, PASSES - 1)
         store(LAST, PASSES - 1)

@@ -35,6 +35,7 @@ FLOPS = 2 * TOKENS * HIDDEN * HEADS * HEAD
 
 BLOCKS_AHEAD = 10
 STEPS = (GROUPS + 1) * PASSES
+SHARED_BLOCKS = 5
 HIDDEN_STEP = (3, 4, 5, 6)
 VECTOR_NOPE_COLUMNS = 48
 
@@ -229,7 +230,7 @@ def tile_multilatentattention_pb_kernel(tc, hidden_states, rope_cos, rope_sin, W
         def scalar_share(s):
             for part, c, g in prepare.get(s, []):
                 if part == "rope":
-                    interleave("scalar", part, c, g, 0, 2 if c == 0 else GROUP_HEADS, 0, ROPE)
+                    interleave("scalar", part, c, g, 0, 2 if s < SHARED_BLOCKS else GROUP_HEADS, 0, ROPE)
                 elif c > 0:
                     interleave("scalar", part, c, g, 0, GROUP_HEADS, VECTOR_NOPE_COLUMNS, NOPE)
 
@@ -237,7 +238,7 @@ def tile_multilatentattention_pb_kernel(tc, hidden_states, rope_cos, rope_sin, W
             for part, c, g in prepare.get(s, []):
                 if part == "nope":
                     interleave("vector", part, c, g, 0, GROUP_HEADS, 0, NOPE if c == 0 else VECTOR_NOPE_COLUMNS)
-                elif c == 0:
+                elif s < SHARED_BLOCKS:
                     interleave("vector", part, c, g, 2, GROUP_HEADS, 0, ROPE)
 
         def rotation(s):
@@ -264,7 +265,7 @@ def tile_multilatentattention_pb_kernel(tc, hidden_states, rope_cos, rope_sin, W
                 second_product(rotation(s)[0], rotation(s)[1])
             if s > PASSES:
                 if rotation(s - 1)[0] < LAST:
-                    copy_unchanged("vector", rotation(s - 1)[0], rotation(s - 1)[1])
+                    copy_unchanged("vector" if s % 2 == 0 else "scalar", rotation(s - 1)[0], rotation(s - 1)[1])
                 store(rotation(s - 1)[0], rotation(s - 1)[1])
             if PASSES - 1 <= s < STEPS - 1:
                 multiply("rope", rotation(s + 1)[0], rotation(s + 1)[1])

@@ -90,11 +90,14 @@ def tile_multilatentattention_pb_kernel(tc, hidden_states, rope_cos, rope_sin, W
         second_table = keep.tile([P, TOKEN_TILES, PAIRS, 2], F32, name="second_table")
         nc.vector.tensor_copy(out=first_table[:, :, :, 0], in_=cos_bf[:])
         nc.vector.tensor_copy(out=first_table[:, :, :, 1], in_=sin_bf[:])
-        nc.scalar.mul(out=second_table[:, :, :, 0], in_=sin_bf[:], mul=-1.0)
-        nc.scalar.copy(out=second_table[:, :, :, 1], in_=cos_bf[:])
-
         identity = keep.tile([P, P], F32, name="identity")
         make_identity(nc, identity[:])
+        nc.gpsimd.tensor_scalar(
+            out=second_table[:, :, :, 0], in0=sin_bf[:], scalar1=-1.0, scalar2=0.0, op0=MULT, op1=ADD
+        )
+        nc.gpsimd.tensor_scalar(
+            out=second_table[:, :, :, 1], in0=cos_bf[:], scalar1=1.0, scalar2=0.0, op0=MULT, op1=ADD
+        )
 
         x_codes = keep.tile([P, TOKEN_TILES, PASSES, P], U32, name="x_codes", align_bytes=64)
         x_scales = keep.tile([P, TOKEN_TILES, PASSES, P], U8, name="x_scales", align_bytes=64)
@@ -155,14 +158,16 @@ def tile_multilatentattention_pb_kernel(tc, hidden_states, rope_cos, rope_sin, W
         second_part = {}
         shape = [P, GROUP_HEADS, PAIRS, 2]
 
-        def multiply(part, c, a):
+        def multiply(part, c, a, first=0, last=PASSES):
             if part == "rope":
-                sums[(part, c, a)] = psum_rope.tile(shape, F32, name="rope_ps")
+                if first == 0:
+                    sums[(part, c, a)] = psum_rope.tile(shape, F32, name="rope_ps")
                 acc = sums[(part, c, a)][:].rearrange("p h i e -> p (h i e)")
             else:
-                sums[(part, c, a)] = psum_small.tile([P, GROUP_HEADS, NOPE], F32, name="small_ps")
-                acc = sums[(part, c, a)][:].rearrange("p h x -> p (h x)")
-            for g in range(PASSES):
+                if first == 0:
+                    sums[(part, c, a)] = psum_small.tile([P, 2, GROUP_HEADS, NOPE], F32, name="small_ps")
+                acc = sums[(part, c, a)][:, 0].rearrange("p h x -> p (h x)")
+            for g in range(first, last):
                 nc.tensor.matmul_mx(
                     out=acc,
                     lhsT=x_codes[:, a, g, :].bitcast(FP8X4),
@@ -205,7 +210,7 @@ def tile_multilatentattention_pb_kernel(tc, hidden_states, rope_cos, rope_sin, W
         def copy_unchanged(engine, c, a):
             new_result(c, a)
             copy = nc.scalar.copy if engine == "scalar" else nc.vector.tensor_copy
-            copy(out=result[(c, a)][:, :, 0:NOPE], in_=sums[("nope", c, a)][:])
+            copy(out=result[(c, a)][:, :, 0:NOPE], in_=sums[("nope", c, a)][:, 0])
 
         gate_word = keep.tile([P, 1], U32, name="gate_word")
 
@@ -219,13 +224,14 @@ def tile_multilatentattention_pb_kernel(tc, hidden_states, rope_cos, rope_sin, W
             )
 
         LAST = GROUPS - 1
+        EARLY_NOPE = 2
         prepare = {}
         for s in range(GROUPS * PASSES):
             prepare[s] = [("rope", s // PASSES, s % PASSES)]
             if s // PASSES < LAST:
                 prepare[s].append(("nope", s // PASSES, s % PASSES))
-        for g in range(PASSES):
-            prepare[LAST * PASSES + g // 2].append(("nope", LAST, g))
+        for g in range(EARLY_NOPE):
+            prepare[LAST * PASSES + g].append(("nope", LAST, g))
 
         def scalar_share(s):
             for part, c, g in prepare.get(s, []):
@@ -248,9 +254,13 @@ def tile_multilatentattention_pb_kernel(tc, hidden_states, rope_cos, rope_sin, W
         for s in range(STEPS):
             for kind, lc, lg in loads[BLOCKS_AHEAD + s : BLOCKS_AHEAD + s + 1]:
                 load(kind, lc, lg)
-            if LAST * PASSES + 3 <= s < STEPS - 1:
-                copy_unchanged("scalar", LAST, s - LAST * PASSES - 3)
+            if s == STEPS - 2 or s == STEPS - 1:
+                for a in range(PASSES // 2):
+                    copy_unchanged("scalar", LAST, (s - STEPS + 2) * 2 + a)
             scalar_share(s + 1)
+            if s == STEPS - PASSES - 1:
+                for g in range(EARLY_NOPE, PASSES):
+                    interleave("scalar", "nope", LAST, g, 0, GROUP_HEADS, 0, NOPE)
             vector_share(s)
             if s in HIDDEN_STEP:
                 quantize_hidden(HIDDEN_STEP.index(s))
@@ -266,13 +276,31 @@ def tile_multilatentattention_pb_kernel(tc, hidden_states, rope_cos, rope_sin, W
             if s > PASSES:
                 if rotation(s - 1)[0] < LAST:
                     copy_unchanged("vector" if s % 2 == 0 else "scalar", rotation(s - 1)[0], rotation(s - 1)[1])
-                store(rotation(s - 1)[0], rotation(s - 1)[1])
-            if PASSES - 1 <= s < STEPS - 1:
+                if rotation(s - 1)[0] < LAST:
+                    store(rotation(s - 1)[0], rotation(s - 1)[1])
+            if s == STEPS - PASSES:
+                for g in range(EARLY_NOPE, PASSES):
+                    quantize("nope", LAST, g)
+            if s == STEPS - 2:
+                store(LAST, 0)
+                store(LAST, 1)
+            if s == STEPS - 1:
+                store(LAST, 2)
+            if PASSES - 1 <= s < STEPS - PASSES - 1:
                 multiply("rope", rotation(s + 1)[0], rotation(s + 1)[1])
-                if rotation(s + 1)[0] < LAST:
-                    multiply("nope", rotation(s + 1)[0], rotation(s + 1)[1])
-            if LAST * PASSES + 1 <= s < LAST * PASSES + 1 + PASSES:
-                multiply("nope", LAST, s - LAST * PASSES - 1)
+                multiply("nope", rotation(s + 1)[0], rotation(s + 1)[1])
+            if s == STEPS - PASSES - 2:
+                for a in range(TOKEN_TILES - 1):
+                    multiply("rope", LAST, a, 0, PASSES - 1)
+            if s == STEPS - PASSES - 1:
+                for a in range(TOKEN_TILES - 1):
+                    multiply("rope", LAST, a, PASSES - 1, PASSES)
+                multiply("rope", LAST, TOKEN_TILES - 1)
+            if s == STEPS - PASSES:
+                for a in range(TOKEN_TILES):
+                    multiply("nope", LAST, a, 0, EARLY_NOPE)
+                for a in range(TOKEN_TILES):
+                    multiply("nope", LAST, a, EARLY_NOPE, PASSES)
             if s + 2 in HIDDEN_STEP:
                 flip_hidden(HIDDEN_STEP.index(s + 2))
         add_products(LAST, PASSES - 1)

@@ -212,10 +212,10 @@ def tile_multilatentattention_pb_kernel(tc, hidden_states, rope_cos, rope_sin, W
             copy = nc.scalar.copy if engine == "scalar" else nc.vector.tensor_copy
             copy(out=result[(c, a)][:, :, 0:NOPE], in_=sums[("nope", c, a)][:, 0])
 
-        gate_word = keep.tile([P, 1], U32, name="gate_word")
+        gate_word = keep.tile([P, 1], F32, name="gate_word")
 
-        def wait_for_codes(c, g):
-            nc.gpsimd.tensor_copy(out=gate_word[:], in_=w_codes[("rope", c)][:, g, 0:1])
+        def open_gate(c, a):
+            nc.vector.tensor_copy(out=gate_word[:], in_=rotated(c, a)[:, 0, 0, 0:1])
 
         def store(c, a):
             nc.sync.dma_start(
@@ -268,7 +268,7 @@ def tile_multilatentattention_pb_kernel(tc, hidden_states, rope_cos, rope_sin, W
                 quantize(part, c, g)
             if s > PASSES:
                 if s < GROUPS * PASSES:
-                    wait_for_codes(s // PASSES, s % PASSES)
+                    open_gate(rotation(s - 1)[0], rotation(s - 1)[1])
                 add_products(rotation(s - 1)[0], rotation(s - 1)[1])
             if s >= PASSES:
                 first_product(rotation(s)[0], rotation(s)[1])

@@ -35,7 +35,9 @@ FLOPS = 2 * TOKENS * HIDDEN * HEADS * HEAD
 
 BLOCKS_AHEAD = 10
 STEPS = (GROUPS + 1) * PASSES
-SHARED_BLOCKS = 5
+WEAVE_FROM = 8
+WEAVE_ENGINE = "vector"
+SHARED_BLOCKS = 6
 HIDDEN_STEP = (3, 4, 5, 6)
 VECTOR_NOPE_COLUMNS = 48
 
@@ -55,7 +57,8 @@ def tile_multilatentattention_pb_kernel(tc, hidden_states, rope_cos, rope_sin, W
         codes_pool = ctx.enter_context(tc.tile_pool(name="codes", bufs=2))
         result_pool = ctx.enter_context(tc.tile_pool(name="result", bufs=8))
         psum_rope = ctx.enter_context(tc.psum_pool(name="psum_rope", bufs=4))
-        psum_small = ctx.enter_context(tc.psum_pool(name="psum_small", bufs=4))
+        psum_small = ctx.enter_context(tc.psum_pool(name="psum_small", bufs=2))
+        psum_weave = ctx.enter_context(tc.psum_pool(name="psum_weave", bufs=2))
         ctx.enter_context(tc.manual_schedule())
 
         cos_bf = keep.tile([P, TOKEN_TILES, PAIRS], BF16, name="cos_bf")
@@ -92,6 +95,8 @@ def tile_multilatentattention_pb_kernel(tc, hidden_states, rope_cos, rope_sin, W
         nc.vector.tensor_copy(out=first_table[:, :, :, 1], in_=sin_bf[:])
         identity = keep.tile([P, P], F32, name="identity")
         make_identity(nc, identity[:])
+        identity_bf = keep.tile([P, P], BF16, name="identity_bf")
+        make_identity(nc, identity_bf[:])
         nc.gpsimd.tensor_scalar(
             out=second_table[:, :, :, 0], in0=sin_bf[:], scalar1=-1.0, scalar2=0.0, op0=MULT, op1=ADD
         )
@@ -142,6 +147,27 @@ def tile_multilatentattention_pb_kernel(tc, hidden_states, rope_cos, rope_sin, W
                 in_=source.rearrange("p j h (c i) -> p h c j i", i=4),
             )
 
+        woven = {}
+
+        def weave(c, g):
+            woven[(c, g)] = psum_weave.tile([P, GROUP_HEADS * NOPE, PACK], BF16, name="woven")
+            by_head = raw[(c, g)][:].rearrange("p j (h x) -> p j h x", x=HEAD)
+            target = woven[(c, g)][:].rearrange("p (h x) j -> p j h x", h=GROUP_HEADS)
+            for h in range(0, GROUP_HEADS, 2):
+                nc.tensor.matmul(
+                    target[:, :, h : h + 2, :], lhsT=identity_bf[:], rhs=by_head[:, :, h : h + 2, 0:NOPE], start=True, stop=True
+                )
+
+        def copy_woven(engine, c, g):
+            w_grouped[("nope", c, g)] = grouped_pool.tile(
+                [P, GROUP_HEADS * NOPE, PACK], BF16, name="nope_grouped", align_bytes=64
+            )
+            copy = nc.scalar.copy if engine == "scalar" else nc.vector.tensor_copy
+            copy(
+                out=w_grouped[("nope", c, g)][:].rearrange("p n j -> p (n j)"),
+                in_=woven[(c, g)][:].rearrange("p n j -> p (n j)"),
+            )
+
         def quantize(part, c, g):
             if g == 0:
                 columns = GROUP_HEADS * WIDTH[part]
@@ -154,6 +180,7 @@ def tile_multilatentattention_pb_kernel(tc, hidden_states, rope_cos, rope_sin, W
             )
 
         sums = {}
+        nope_bank = {}
         result = {}
         second_part = {}
         shape = [P, GROUP_HEADS, PAIRS, 2]
@@ -165,8 +192,10 @@ def tile_multilatentattention_pb_kernel(tc, hidden_states, rope_cos, rope_sin, W
                 acc = sums[(part, c, a)][:].rearrange("p h i e -> p (h i e)")
             else:
                 if first == 0:
-                    sums[(part, c, a)] = psum_small.tile([P, 2, GROUP_HEADS, NOPE], F32, name="small_ps")
-                acc = sums[(part, c, a)][:, 0].rearrange("p h x -> p (h x)")
+                    if a % 2 == 0:
+                        nope_bank[c] = psum_small.tile([P, 2, GROUP_HEADS, NOPE], F32, name="small_ps")
+                    sums[(part, c, a)] = nope_bank[c][:, a % 2]
+                acc = sums[(part, c, a)].rearrange("p h x -> p (h x)")
             for g in range(first, last):
                 nc.tensor.matmul_mx(
                     out=acc,
@@ -210,7 +239,7 @@ def tile_multilatentattention_pb_kernel(tc, hidden_states, rope_cos, rope_sin, W
         def copy_unchanged(engine, c, a):
             new_result(c, a)
             copy = nc.scalar.copy if engine == "scalar" else nc.vector.tensor_copy
-            copy(out=result[(c, a)][:, :, 0:NOPE], in_=sums[("nope", c, a)][:, 0])
+            copy(out=result[(c, a)][:, :, 0:NOPE], in_=sums[("nope", c, a)])
 
         gate_word = keep.tile([P, 1], F32, name="gate_word")
 
@@ -237,13 +266,17 @@ def tile_multilatentattention_pb_kernel(tc, hidden_states, rope_cos, rope_sin, W
             for part, c, g in prepare.get(s, []):
                 if part == "rope":
                     interleave("scalar", part, c, g, 0, 2 if s < SHARED_BLOCKS else GROUP_HEADS, 0, ROPE)
+                elif s >= WEAVE_FROM:
+                    if WEAVE_ENGINE == "scalar":
+                        copy_woven("scalar", c, g)
                 elif c > 0:
                     interleave("scalar", part, c, g, 0, GROUP_HEADS, VECTOR_NOPE_COLUMNS, NOPE)
 
         def vector_share(s):
             for part, c, g in prepare.get(s, []):
                 if part == "nope":
-                    interleave("vector", part, c, g, 0, GROUP_HEADS, 0, NOPE if c == 0 else VECTOR_NOPE_COLUMNS)
+                    if s < WEAVE_FROM:
+                        interleave("vector", part, c, g, 0, GROUP_HEADS, 0, NOPE if c == 0 else VECTOR_NOPE_COLUMNS)
                 elif s < SHARED_BLOCKS:
                     interleave("vector", part, c, g, 2, GROUP_HEADS, 0, ROPE)
 
@@ -275,9 +308,12 @@ def tile_multilatentattention_pb_kernel(tc, hidden_states, rope_cos, rope_sin, W
                 second_product(rotation(s)[0], rotation(s)[1])
             if s > PASSES:
                 if rotation(s - 1)[0] < LAST:
-                    copy_unchanged("vector" if s % 2 == 0 else "scalar", rotation(s - 1)[0], rotation(s - 1)[1])
+                    copy_unchanged("scalar", rotation(s - 1)[0], rotation(s - 1)[1])
                 if rotation(s - 1)[0] < LAST:
                     store(rotation(s - 1)[0], rotation(s - 1)[1])
+            for part, c, g in prepare.get(s + 1, []):
+                if part == "nope" and s + 1 >= WEAVE_FROM and WEAVE_ENGINE == "vector":
+                    copy_woven("vector", c, g)
             if s == STEPS - PASSES:
                 for g in range(EARLY_NOPE, PASSES):
                     quantize("nope", LAST, g)
@@ -288,7 +324,9 @@ def tile_multilatentattention_pb_kernel(tc, hidden_states, rope_cos, rope_sin, W
                 store(LAST, 2)
             if PASSES - 1 <= s < STEPS - PASSES - 1:
                 multiply("rope", rotation(s + 1)[0], rotation(s + 1)[1])
-                multiply("nope", rotation(s + 1)[0], rotation(s + 1)[1])
+                if rotation(s + 1)[1] % 2 == 1:
+                    multiply("nope", rotation(s + 1)[0], rotation(s + 1)[1] - 1)
+                    multiply("nope", rotation(s + 1)[0], rotation(s + 1)[1])
             if s == STEPS - PASSES - 2:
                 for a in range(TOKEN_TILES - 1):
                     multiply("rope", LAST, a, 0, PASSES - 1)
@@ -298,10 +336,11 @@ def tile_multilatentattention_pb_kernel(tc, hidden_states, rope_cos, rope_sin, W
                 multiply("rope", LAST, TOKEN_TILES - 1)
             if s == STEPS - PASSES:
                 for a in range(TOKEN_TILES):
-                    multiply("nope", LAST, a, 0, EARLY_NOPE)
-                for a in range(TOKEN_TILES):
-                    multiply("nope", LAST, a, EARLY_NOPE, PASSES)
+                    multiply("nope", LAST, a)
             if s + 2 in HIDDEN_STEP:
                 flip_hidden(HIDDEN_STEP.index(s + 2))
+            for part, c, g in prepare.get(s + 2, []):
+                if part == "nope" and s + 2 >= WEAVE_FROM:
+                    weave(c, g)
         add_products(LAST, PASSES - 1)
         store(LAST, PASSES - 1)

@@ -35,11 +35,21 @@ FLOPS = 2 * TOKENS * HIDDEN * HEADS * HEAD
 
 BLOCKS_AHEAD = 10
 STEPS = (GROUPS + 1) * PASSES
-WEAVE_FROM = 8
-WEAVE_ENGINE = "vector"
-SHARED_BLOCKS = 6
+WEAVE_FROM = 7
+EARLY_ROTATIONS = False
+TABLES_AFTER = 0
+TABLES_STEP = 3
+SPREAD = False
+PROGRESSIVE = False
+COPY_AT = 0
+FIRST_SPLIT = False
+SPLIT_LAST = True
+HIDDEN_FIRST = False
+DEFER_WEAVE = False
+VADD = 2
+SCALAR_HEADS = {s: 3 if s < 3 else 2 for s in range(6)}
 HIDDEN_STEP = (3, 4, 5, 6)
-VECTOR_NOPE_COLUMNS = 48
+SCALAR_NOPE = {5: 0}
 
 
 def tile_multilatentattention_pb_kernel(tc, hidden_states, rope_cos, rope_sin, Wq, out):
@@ -63,8 +73,12 @@ def tile_multilatentattention_pb_kernel(tc, hidden_states, rope_cos, rope_sin, W
 
         cos_bf = keep.tile([P, TOKEN_TILES, PAIRS], BF16, name="cos_bf")
         sin_bf = keep.tile([P, TOKEN_TILES, PAIRS], BF16, name="sin_bf")
-        nc.sync.dma_start(out=cos_bf[:], in_=cos_view)
-        nc.sync.dma_start(out=sin_bf[:], in_=sin_view)
+        def load_tables():
+            nc.sync.dma_start(out=cos_bf[:], in_=cos_view)
+            nc.sync.dma_start(out=sin_bf[:], in_=sin_view)
+
+        if TABLES_AFTER == 0:
+            load_tables()
 
         x_sb = {}
         raw = {}
@@ -75,10 +89,12 @@ def tile_multilatentattention_pb_kernel(tc, hidden_states, rope_cos, rope_sin, W
                 nc.sync.dma_start(out=x_sb[c][:], in_=hidden_view[:, c, :])
             else:
                 raw[(c, g)] = keep.tile([P, PACK, GROUP_COLS], BF16, name="raw_%d_%d" % (c, g))
-                nc.sync.dma_start(
-                    out=raw[(c, g)][:],
-                    in_=w_view[g][:, :, c * GROUP_COLS : (c + 1) * GROUP_COLS],
-                )
+                step = GROUP_COLS // 2 if FIRST_SPLIT and (c, g) == (0, 0) else GROUP_COLS
+                for n0 in range(0, GROUP_COLS, step):
+                    nc.sync.dma_start(
+                        out=raw[(c, g)][:, :, n0 : n0 + step],
+                        in_=w_view[g][:, :, c * GROUP_COLS + n0 : c * GROUP_COLS + n0 + step],
+                    )
 
         loads = []
         for s in range(GROUPS * PASSES):
@@ -86,24 +102,30 @@ def tile_multilatentattention_pb_kernel(tc, hidden_states, rope_cos, rope_sin, W
             for a in range(TOKEN_TILES):
                 if HIDDEN_STEP[a] - 1 == s:
                     loads.append(("x", a, 0))
-        for kind, c, g in loads[0:BLOCKS_AHEAD]:
+        for i, (kind, c, g) in enumerate(loads[0:BLOCKS_AHEAD]):
+            if TABLES_AFTER and i == TABLES_AFTER:
+                load_tables()
             load(kind, c, g)
 
         first_table = keep.tile([P, TOKEN_TILES, PAIRS, 2], F32, name="first_table")
         second_table = keep.tile([P, TOKEN_TILES, PAIRS, 2], F32, name="second_table")
-        nc.vector.tensor_copy(out=first_table[:, :, :, 0], in_=cos_bf[:])
-        nc.vector.tensor_copy(out=first_table[:, :, :, 1], in_=sin_bf[:])
+        def make_tables():
+            nc.vector.tensor_copy(out=first_table[:, :, :, 0], in_=cos_bf[:])
+            nc.vector.tensor_copy(out=first_table[:, :, :, 1], in_=sin_bf[:])
+            nc.gpsimd.tensor_scalar(
+                out=second_table[:, :, :, 0], in0=sin_bf[:], scalar1=-1.0, scalar2=0.0, op0=MULT, op1=ADD
+            )
+            nc.gpsimd.tensor_scalar(
+                out=second_table[:, :, :, 1], in0=cos_bf[:], scalar1=1.0, scalar2=0.0, op0=MULT, op1=ADD
+            )
+
+        if TABLES_AFTER == 0:
+            make_tables()
+
         identity = keep.tile([P, P], F32, name="identity")
         make_identity(nc, identity[:])
         identity_bf = keep.tile([P, P], BF16, name="identity_bf")
         make_identity(nc, identity_bf[:])
-        nc.gpsimd.tensor_scalar(
-            out=second_table[:, :, :, 0], in0=sin_bf[:], scalar1=-1.0, scalar2=0.0, op0=MULT, op1=ADD
-        )
-        nc.gpsimd.tensor_scalar(
-            out=second_table[:, :, :, 1], in0=cos_bf[:], scalar1=1.0, scalar2=0.0, op0=MULT, op1=ADD
-        )
-
         x_codes = keep.tile([P, TOKEN_TILES, PASSES, P], U32, name="x_codes", align_bytes=64)
         x_scales = keep.tile([P, TOKEN_TILES, PASSES, P], U8, name="x_scales", align_bytes=64)
         x_grouped = {}
@@ -192,9 +214,15 @@ def tile_multilatentattention_pb_kernel(tc, hidden_states, rope_cos, rope_sin, W
                 acc = sums[(part, c, a)][:].rearrange("p h i e -> p (h i e)")
             else:
                 if first == 0:
-                    if a % 2 == 0:
+                    if PROGRESSIVE and c == LAST:
+                        if a < 2:
+                            bank = psum_small.tile([P, 2, GROUP_HEADS, NOPE], F32, name="small_ps")
+                        else:
+                            bank = psum_weave.tile([P, 2, GROUP_HEADS, NOPE], F32, name="woven")
+                        nope_bank[c] = bank
+                    elif a % 2 == 0:
                         nope_bank[c] = psum_small.tile([P, 2, GROUP_HEADS, NOPE], F32, name="small_ps")
-                    sums[(part, c, a)] = nope_bank[c][:, a % 2]
+                    sums[(part, c, a)] = nope_bank[c][:, 0 if PROGRESSIVE and c == LAST else a % 2]
                 acc = sums[(part, c, a)].rearrange("p h x -> p (h x)")
             for g in range(first, last):
                 nc.tensor.matmul_mx(
@@ -214,27 +242,32 @@ def tile_multilatentattention_pb_kernel(tc, hidden_states, rope_cos, rope_sin, W
         def rotated(c, a):
             return result[(c, a)][:, :, NOPE:HEAD].rearrange("p h (i e) -> p h i e", e=2)
 
-        def first_product(c, a):
+        def first_product(c, a, h0=0, h1=GROUP_HEADS):
             new_result(c, a)
+            part = [P, h1 - h0, PAIRS, 2]
             nc.vector.tensor_tensor(
-                out=rotated(c, a),
-                in0=sums[("rope", c, a)][:, :, :, 0:1].to_broadcast(shape),
-                in1=first_table[:, a].unsqueeze(1).to_broadcast(shape),
+                out=rotated(c, a)[:, h0:h1],
+                in0=sums[("rope", c, a)][:, h0:h1, :, 0:1].to_broadcast(part),
+                in1=first_table[:, a].unsqueeze(1).to_broadcast(part),
                 op=MULT,
             )
 
-        def second_product(c, a):
-            second_part[(c, a)] = result_pool.tile(shape, F32, name="second_part", bufs=3)
+        def second_product(c, a, h0=0, h1=GROUP_HEADS):
+            if h0 == 0:
+                second_part[(c, a)] = result_pool.tile(shape, F32, name="second_part", bufs=3)
+            part = [P, h1 - h0, PAIRS, 2]
             nc.vector.tensor_tensor(
-                out=second_part[(c, a)][:],
-                in0=sums[("rope", c, a)][:, :, :, 1:2].to_broadcast(shape),
-                in1=second_table[:, a].unsqueeze(1).to_broadcast(shape),
+                out=second_part[(c, a)][:, h0:h1],
+                in0=sums[("rope", c, a)][:, h0:h1, :, 1:2].to_broadcast(part),
+                in1=second_table[:, a].unsqueeze(1).to_broadcast(part),
                 op=MULT,
             )
 
-        def add_products(c, a):
-            engine = nc.vector if (c == GROUPS - 1 and a == PASSES - 1) else nc.gpsimd
-            engine.tensor_tensor(out=rotated(c, a), in0=rotated(c, a), in1=second_part[(c, a)][:], op=ADD)
+        def add_products(c, a, h0=0, h1=GROUP_HEADS):
+            engine = nc.vector if (c == GROUPS - 1 and a >= PASSES - VADD) else nc.gpsimd
+            engine.tensor_tensor(
+                out=rotated(c, a)[:, h0:h1], in0=rotated(c, a)[:, h0:h1], in1=second_part[(c, a)][:, h0:h1], op=ADD
+            )
 
         def copy_unchanged(engine, c, a):
             new_result(c, a)
@@ -246,10 +279,10 @@ def tile_multilatentattention_pb_kernel(tc, hidden_states, rope_cos, rope_sin, W
         def open_gate(c, a):
             nc.vector.tensor_copy(out=gate_word[:], in_=rotated(c, a)[:, 0, 0, 0:1])
 
-        def store(c, a):
+        def store(c, a, h0=0, h1=GROUP_HEADS):
             nc.sync.dma_start(
-                out=out_view[:, a, c * GROUP_COLS : (c + 1) * GROUP_COLS],
-                in_=result[(c, a)][:].rearrange("p h d -> p (h d)"),
+                out=out_view[:, a, c * GROUP_COLS + h0 * HEAD : c * GROUP_COLS + h1 * HEAD],
+                in_=result[(c, a)][:, h0:h1].rearrange("p h d -> p (h d)"),
             )
 
         LAST = GROUPS - 1
@@ -265,59 +298,79 @@ def tile_multilatentattention_pb_kernel(tc, hidden_states, rope_cos, rope_sin, W
         def scalar_share(s):
             for part, c, g in prepare.get(s, []):
                 if part == "rope":
-                    interleave("scalar", part, c, g, 0, 2 if s < SHARED_BLOCKS else GROUP_HEADS, 0, ROPE)
-                elif s >= WEAVE_FROM:
-                    if WEAVE_ENGINE == "scalar":
-                        copy_woven("scalar", c, g)
-                elif c > 0:
-                    interleave("scalar", part, c, g, 0, GROUP_HEADS, VECTOR_NOPE_COLUMNS, NOPE)
+                    interleave("scalar", part, c, g, 0, SCALAR_HEADS.get(s, GROUP_HEADS), 0, ROPE)
+                elif s in SCALAR_NOPE:
+                    interleave("scalar", part, c, g, 0, GROUP_HEADS, SCALAR_NOPE[s], NOPE)
 
         def vector_share(s):
+            if FIRST_SPLIT and s == 0:
+                interleave("vector", "nope", 0, 0, 0, 2, 0, NOPE)
+                interleave("vector", "rope", 0, 0, 2, 4, 0, ROPE)
+                interleave("vector", "nope", 0, 0, 2, 4, 0, NOPE)
+                return
             for part, c, g in prepare.get(s, []):
                 if part == "nope":
-                    if s < WEAVE_FROM:
-                        interleave("vector", part, c, g, 0, GROUP_HEADS, 0, NOPE if c == 0 else VECTOR_NOPE_COLUMNS)
-                elif s < SHARED_BLOCKS:
-                    interleave("vector", part, c, g, 2, GROUP_HEADS, 0, ROPE)
+                    if s < WEAVE_FROM and SCALAR_NOPE.get(s, NOPE) > 0:
+                        interleave("vector", part, c, g, 0, GROUP_HEADS, 0, SCALAR_NOPE.get(s, NOPE))
+                elif SCALAR_HEADS.get(s, GROUP_HEADS) < GROUP_HEADS:
+                    interleave("vector", part, c, g, SCALAR_HEADS[s], GROUP_HEADS, 0, ROPE)
 
         def rotation(s):
             return s // PASSES - 1, s % PASSES
 
-        scalar_share(0)
-        for s in range(STEPS):
-            for kind, lc, lg in loads[BLOCKS_AHEAD + s : BLOCKS_AHEAD + s + 1]:
-                load(kind, lc, lg)
-            if s == STEPS - 2 or s == STEPS - 1:
-                for a in range(PASSES // 2):
-                    copy_unchanged("scalar", LAST, (s - STEPS + 2) * 2 + a)
-            scalar_share(s + 1)
-            if s == STEPS - PASSES - 1:
-                for g in range(EARLY_NOPE, PASSES):
-                    interleave("scalar", "nope", LAST, g, 0, GROUP_HEADS, 0, NOPE)
-            vector_share(s)
-            if s in HIDDEN_STEP:
-                quantize_hidden(HIDDEN_STEP.index(s))
-            for part, c, g in prepare.get(s, []):
-                quantize(part, c, g)
+        def rotate(s):
             if s > PASSES:
                 if s < GROUPS * PASSES:
                     open_gate(rotation(s - 1)[0], rotation(s - 1)[1])
                 add_products(rotation(s - 1)[0], rotation(s - 1)[1])
-            if s >= PASSES:
+            if not (SPLIT_LAST and s == STEPS - 1):
                 first_product(rotation(s)[0], rotation(s)[1])
                 second_product(rotation(s)[0], rotation(s)[1])
             if s > PASSES:
                 if rotation(s - 1)[0] < LAST:
                     copy_unchanged("scalar", rotation(s - 1)[0], rotation(s - 1)[1])
-                if rotation(s - 1)[0] < LAST:
                     store(rotation(s - 1)[0], rotation(s - 1)[1])
+
+        scalar_share(0)
+        for s in range(STEPS):
+            for kind, lc, lg in loads[BLOCKS_AHEAD + s : BLOCKS_AHEAD + s + 1]:
+                load(kind, lc, lg)
+            if COPY_AT == 0 and (s == STEPS - 2 or s == STEPS - 1):
+                for a in range(PASSES // 2):
+                    copy_unchanged("scalar", LAST, (s - STEPS + 2) * 2 + a)
+            if COPY_AT and s == STEPS - 1:
+                for a in range(PASSES):
+                    copy_unchanged("scalar", LAST, a)
+            scalar_share(s + 1)
+            if s == STEPS - PASSES - 1:
+                for g in range(EARLY_NOPE, PASSES):
+                    if not DEFER_WEAVE:
+                        interleave("scalar", "nope", LAST, g, 0, GROUP_HEADS, 0, NOPE)
+            if TABLES_AFTER and s == TABLES_STEP:
+                make_tables()
+            if EARLY_ROTATIONS and PASSES <= s < 2 * PASSES:
+                rotate(s)
+            if HIDDEN_FIRST and s in HIDDEN_STEP:
+                quantize_hidden(HIDDEN_STEP.index(s))
+            vector_share(s)
+            if not HIDDEN_FIRST and s in HIDDEN_STEP:
+                quantize_hidden(HIDDEN_STEP.index(s))
+            for part, c, g in prepare.get(s, []):
+                quantize(part, c, g)
+            if s >= (2 * PASSES if EARLY_ROTATIONS else PASSES):
+                rotate(s)
             for part, c, g in prepare.get(s + 1, []):
-                if part == "nope" and s + 1 >= WEAVE_FROM and WEAVE_ENGINE == "vector":
+                if part == "nope" and s + 1 >= WEAVE_FROM:
                     copy_woven("vector", c, g)
-            if s == STEPS - PASSES:
+            if s == STEPS - PASSES and not SPREAD:
                 for g in range(EARLY_NOPE, PASSES):
                     quantize("nope", LAST, g)
-            if s == STEPS - 2:
+            if SPREAD and STEPS - PASSES <= s < STEPS - EARLY_NOPE:
+                quantize("nope", LAST, EARLY_NOPE + s - STEPS + PASSES)
+            if COPY_AT == 0 and s == STEPS - 2:
+                store(LAST, 0)
+                store(LAST, 1)
+            if COPY_AT and s == STEPS - 1:
                 store(LAST, 0)
                 store(LAST, 1)
             if s == STEPS - 1:
@@ -334,7 +387,15 @@ def tile_multilatentattention_pb_kernel(tc, hidden_states, rope_cos, rope_sin, W
                 for a in range(TOKEN_TILES - 1):
                     multiply("rope", LAST, a, PASSES - 1, PASSES)
                 multiply("rope", LAST, TOKEN_TILES - 1)
-            if s == STEPS - PASSES:
+                for g in range(EARLY_NOPE, PASSES):
+                    if DEFER_WEAVE:
+                        weave(LAST, g)
+                        copy_woven("scalar", LAST, g)
+            if PROGRESSIVE and STEPS - PASSES <= s < STEPS - EARLY_NOPE:
+                g = EARLY_NOPE + s - STEPS + PASSES
+                for a in range(TOKEN_TILES):
+                    multiply("nope", LAST, a, 0 if g == EARLY_NOPE else g, g + 1)
+            if not PROGRESSIVE and s == STEPS - PASSES + (1 if SPREAD else 0):
                 for a in range(TOKEN_TILES):
                     multiply("nope", LAST, a)
             if s + 2 in HIDDEN_STEP:
@@ -342,5 +403,13 @@ def tile_multilatentattention_pb_kernel(tc, hidden_states, rope_cos, rope_sin, W
             for part, c, g in prepare.get(s + 2, []):
                 if part == "nope" and s + 2 >= WEAVE_FROM:
                     weave(c, g)
-        add_products(LAST, PASSES - 1)
-        store(LAST, PASSES - 1)
+        if SPLIT_LAST:
+            for h0 in (0, 2):
+                first_product(LAST, PASSES - 1, h0, h0 + 2)
+                second_product(LAST, PASSES - 1, h0, h0 + 2)
+            for h0 in (0, 2):
+                add_products(LAST, PASSES - 1, h0, h0 + 2)
+                store(LAST, PASSES - 1, h0, h0 + 2)
+        else:
+            add_products(LAST, PASSES - 1)
+            store(LAST, PASSES - 1)

from contextlib import ExitStack

import concourse.mybir as mybir
from concourse.masks import make_identity

F32 = mybir.dt.float32
BF16 = mybir.dt.bfloat16
U32 = mybir.dt.uint32
U8 = mybir.dt.uint8
FP8X4 = mybir.dt.float8_e4m3fn_x4
MULT = mybir.AluOpType.mult
ADD = mybir.AluOpType.add

P = 128
PACK = 4
K_PASS = P * PACK

TOKENS = 512
HIDDEN = 2048
HEADS = 16
NOPE = 64
ROPE = 128
HEAD = NOPE + ROPE
PAIRS = ROPE // 2

TOKEN_TILES = TOKENS // P
PASSES = HIDDEN // K_PASS
GROUP_HEADS = 4
GROUPS = HEADS // GROUP_HEADS
GROUP_COLS = GROUP_HEADS * HEAD
WIDTH = {"rope": ROPE, "nope": NOPE}
FIRST = {"rope": NOPE, "nope": 0}

FLOPS = 2 * TOKENS * HIDDEN * HEADS * HEAD

BLOCKS_AHEAD = 10
STEPS = (GROUPS + 1) * PASSES
WEAVE_FROM = 7
EARLY_ROTATIONS = False
TABLES_AFTER = 0
TABLES_STEP = 3
SPREAD = False
PROGRESSIVE = False
COPY_AT = 0
FIRST_SPLIT = False
SPLIT_LAST = True
HIDDEN_FIRST = False
DEFER_WEAVE = False
VADD = 2
SCALAR_HEADS = {s: 3 if s < 3 else 2 for s in range(6)}
HIDDEN_STEP = (3, 4, 5, 6)
SCALAR_NOPE = {5: 0}


def tile_multilatentattention_pb_kernel(tc, hidden_states, rope_cos, rope_sin, Wq, out):
    nc = tc.nc

    hidden_view = hidden_states.rearrange("b (p a) k -> p (b a) k", a=TOKEN_TILES)
    cos_view = rope_cos.rearrange("(p a) i -> p a i", a=TOKEN_TILES)
    sin_view = rope_sin.rearrange("(p a) i -> p a i", a=TOKEN_TILES)
    out_view = out.rearrange("b (p a) h d -> p (b a) (h d)", a=TOKEN_TILES)
    w_view = Wq.rearrange("(g p j) n -> g p j n", p=P, j=PACK)

    with ExitStack() as ctx:
        keep = ctx.enter_context(tc.tile_pool(name="keep", bufs=1))
        grouped_pool = ctx.enter_context(tc.tile_pool(name="grouped", bufs=4))
        codes_pool = ctx.enter_context(tc.tile_pool(name="codes", bufs=2))
        result_pool = ctx.enter_context(tc.tile_pool(name="result", bufs=8))
        psum_rope = ctx.enter_context(tc.psum_pool(name="psum_rope", bufs=4))
        psum_small = ctx.enter_context(tc.psum_pool(name="psum_small", bufs=2))
        psum_weave = ctx.enter_context(tc.psum_pool(name="psum_weave", bufs=2))
        ctx.enter_context(tc.manual_schedule())

        cos_bf = keep.tile([P, TOKEN_TILES, PAIRS], BF16, name="cos_bf")
        sin_bf = keep.tile([P, TOKEN_TILES, PAIRS], BF16, name="sin_bf")
        def load_tables():
            nc.sync.dma_start(out=cos_bf[:], in_=cos_view)
            nc.sync.dma_start(out=sin_bf[:], in_=sin_view)

        if TABLES_AFTER == 0:
            load_tables()

        x_sb = {}
        raw = {}

        def load(kind, c, g):
            if kind == "x":
                x_sb[c] = keep.tile([P, HIDDEN], BF16, name="x_sb_%d" % c)
                nc.sync.dma_start(out=x_sb[c][:], in_=hidden_view[:, c, :])
            else:
                raw[(c, g)] = keep.tile([P, PACK, GROUP_COLS], BF16, name="raw_%d_%d" % (c, g))
                step = GROUP_COLS // 2 if FIRST_SPLIT and (c, g) == (0, 0) else GROUP_COLS
                for n0 in range(0, GROUP_COLS, step):
                    nc.sync.dma_start(
                        out=raw[(c, g)][:, :, n0 : n0 + step],
                        in_=w_view[g][:, :, c * GROUP_COLS + n0 : c * GROUP_COLS + n0 + step],
                    )

        loads = []
        for s in range(GROUPS * PASSES):
            loads.append(("w", s // PASSES, s % PASSES))
            for a in range(TOKEN_TILES):
                if HIDDEN_STEP[a] - 1 == s:
                    loads.append(("x", a, 0))
        for i, (kind, c, g) in enumerate(loads[0:BLOCKS_AHEAD]):
            if TABLES_AFTER and i == TABLES_AFTER:
                load_tables()
            load(kind, c, g)

        first_table = keep.tile([P, TOKEN_TILES, PAIRS, 2], F32, name="first_table")
        second_table = keep.tile([P, TOKEN_TILES, PAIRS, 2], F32, name="second_table")
        def make_tables():
            nc.vector.tensor_copy(out=first_table[:, :, :, 0], in_=cos_bf[:])
            nc.vector.tensor_copy(out=first_table[:, :, :, 1], in_=sin_bf[:])
            nc.gpsimd.tensor_scalar(
                out=second_table[:, :, :, 0], in0=sin_bf[:], scalar1=-1.0, scalar2=0.0, op0=MULT, op1=ADD
            )
            nc.gpsimd.tensor_scalar(
                out=second_table[:, :, :, 1], in0=cos_bf[:], scalar1=1.0, scalar2=0.0, op0=MULT, op1=ADD
            )

        if TABLES_AFTER == 0:
            make_tables()

        identity = keep.tile([P, P], F32, name="identity")
        make_identity(nc, identity[:])
        identity_bf = keep.tile([P, P], BF16, name="identity_bf")
        make_identity(nc, identity_bf[:])
        x_codes = keep.tile([P, TOKEN_TILES, PASSES, P], U32, name="x_codes", align_bytes=64)
        x_scales = keep.tile([P, TOKEN_TILES, PASSES, P], U8, name="x_scales", align_bytes=64)
        x_grouped = {}

        def flip_hidden(a):
            words = x_sb[a][:].bitcast(F32).rearrange("p (g q u) -> p g u q", q=P, u=2)
            x_grouped[a] = grouped_pool.tile([P, PASSES, P, PACK], BF16, name="x_grouped", align_bytes=64)
            x_grouped_words = x_grouped[a][:].bitcast(F32)
            for half in range(2):
                flipped = psum_rope.tile([P, 2, 2, P], F32, name="rope_ps")
                for gg in range(2):
                    for u in range(2):
                        nc.tensor.transpose(flipped[:, gg, u, :], words[:, 2 * half + gg, u, :], identity[:])
                nc.scalar.copy(
                    out=x_grouped_words[:, 2 * half : 2 * half + 2],
                    in_=flipped[:].rearrange("p g u t -> p g t u"),
                )

        def quantize_hidden(a):
            nc.vector.quantize_mx(
                out=x_codes[:, a].rearrange("p g t -> p (g t)").bitcast(FP8X4),
                scales=x_scales[:, a].rearrange("p g t -> p (g t)"),
                in_=x_grouped[a][:].rearrange("p g t j -> p (g t j)"),
            )

        w_grouped = {}
        w_codes = {}
        w_scales = {}

        def interleave(engine, part, c, g, h0, h1, x0, x1):
            if (part, c, g) not in w_grouped:
                w_grouped[(part, c, g)] = grouped_pool.tile(
                    [P, GROUP_HEADS * WIDTH[part], PACK], BF16, name=part + "_grouped", align_bytes=64
                )
            by_head = raw[(c, g)][:].rearrange("p j (h x) -> p j h x", x=HEAD)
            source = by_head[:, :, h0:h1, FIRST[part] + x0 : FIRST[part] + x1]
            target = w_grouped[(part, c, g)][:].rearrange("p (h x) j -> p h x j", h=GROUP_HEADS)[:, h0:h1, x0:x1, :]
            copy = nc.scalar.copy if engine == "scalar" else nc.vector.tensor_copy
            copy(
                out=target.rearrange("p h (c i) j -> p h c j i", i=4),
                in_=source.rearrange("p j h (c i) -> p h c j i", i=4),
            )

        woven = {}

        def weave(c, g):
            woven[(c, g)] = psum_weave.tile([P, GROUP_HEADS * NOPE, PACK], BF16, name="woven")
            by_head = raw[(c, g)][:].rearrange("p j (h x) -> p j h x", x=HEAD)
            target = woven[(c, g)][:].rearrange("p (h x) j -> p j h x", h=GROUP_HEADS)
            for h in range(0, GROUP_HEADS, 2):
                nc.tensor.matmul(
                    target[:, :, h : h + 2, :], lhsT=identity_bf[:], rhs=by_head[:, :, h : h + 2, 0:NOPE], start=True, stop=True
                )

        def copy_woven(engine, c, g):
            w_grouped[("nope", c, g)] = grouped_pool.tile(
                [P, GROUP_HEADS * NOPE, PACK], BF16, name="nope_grouped", align_bytes=64
            )
            copy = nc.scalar.copy if engine == "scalar" else nc.vector.tensor_copy
            copy(
                out=w_grouped[("nope", c, g)][:].rearrange("p n j -> p (n j)"),
                in_=woven[(c, g)][:].rearrange("p n j -> p (n j)"),
            )

        def quantize(part, c, g):
            if g == 0:
                columns = GROUP_HEADS * WIDTH[part]
                w_codes[(part, c)] = codes_pool.tile([P, PASSES, columns], U32, name=part + "_codes", align_bytes=64)
                w_scales[(part, c)] = codes_pool.tile([P, PASSES, columns], U8, name=part + "_scales", align_bytes=64)
            nc.vector.quantize_mx(
                out=w_codes[(part, c)][:, g, :].bitcast(FP8X4),
                scales=w_scales[(part, c)][:, g, :],
                in_=w_grouped[(part, c, g)][:].rearrange("p n j -> p (n j)"),
            )

        sums = {}
        nope_bank = {}
        result = {}
        second_part = {}
        shape = [P, GROUP_HEADS, PAIRS, 2]

        def multiply(part, c, a, first=0, last=PASSES):
            if part == "rope":
                if first == 0:
                    sums[(part, c, a)] = psum_rope.tile(shape, F32, name="rope_ps")
                acc = sums[(part, c, a)][:].rearrange("p h i e -> p (h i e)")
            else:
                if first == 0:
                    if PROGRESSIVE and c == LAST:
                        if a < 2:
                            bank = psum_small.tile([P, 2, GROUP_HEADS, NOPE], F32, name="small_ps")
                        else:
                            bank = psum_weave.tile([P, 2, GROUP_HEADS, NOPE], F32, name="woven")
                        nope_bank[c] = bank
                    elif a % 2 == 0:
                        nope_bank[c] = psum_small.tile([P, 2, GROUP_HEADS, NOPE], F32, name="small_ps")
                    sums[(part, c, a)] = nope_bank[c][:, 0 if PROGRESSIVE and c == LAST else a % 2]
                acc = sums[(part, c, a)].rearrange("p h x -> p (h x)")
            for g in range(first, last):
                nc.tensor.matmul_mx(
                    out=acc,
                    lhsT=x_codes[:, a, g, :].bitcast(FP8X4),
                    lhsT_scale=x_scales[:, a, g, :],
                    rhs=w_codes[(part, c)][:, g, :].bitcast(FP8X4),
                    rhs_scale=w_scales[(part, c)][:, g, :],
                    start=(g == 0),
                    stop=(g == PASSES - 1),
                )

        def new_result(c, a):
            if (c, a) not in result:
                result[(c, a)] = result_pool.tile([P, GROUP_HEADS, HEAD], F32, name="result")

        def rotated(c, a):
            return result[(c, a)][:, :, NOPE:HEAD].rearrange("p h (i e) -> p h i e", e=2)

        def first_product(c, a, h0=0, h1=GROUP_HEADS):
            new_result(c, a)
            part = [P, h1 - h0, PAIRS, 2]
            nc.vector.tensor_tensor(
                out=rotated(c, a)[:, h0:h1],
                in0=sums[("rope", c, a)][:, h0:h1, :, 0:1].to_broadcast(part),
                in1=first_table[:, a].unsqueeze(1).to_broadcast(part),
                op=MULT,
            )

        def second_product(c, a, h0=0, h1=GROUP_HEADS):
            if h0 == 0:
                second_part[(c, a)] = result_pool.tile(shape, F32, name="second_part", bufs=3)
            part = [P, h1 - h0, PAIRS, 2]
            nc.vector.tensor_tensor(
                out=second_part[(c, a)][:, h0:h1],
                in0=sums[("rope", c, a)][:, h0:h1, :, 1:2].to_broadcast(part),
                in1=second_table[:, a].unsqueeze(1).to_broadcast(part),
                op=MULT,
            )

        def add_products(c, a, h0=0, h1=GROUP_HEADS):
            engine = nc.vector if (c == GROUPS - 1 and a >= PASSES - VADD) else nc.gpsimd
            engine.tensor_tensor(
                out=rotated(c, a)[:, h0:h1], in0=rotated(c, a)[:, h0:h1], in1=second_part[(c, a)][:, h0:h1], op=ADD
            )

        def copy_unchanged(engine, c, a):
            new_result(c, a)
            copy = nc.scalar.copy if engine == "scalar" else nc.vector.tensor_copy
            copy(out=result[(c, a)][:, :, 0:NOPE], in_=sums[("nope", c, a)])

        gate_word = keep.tile([P, 1], F32, name="gate_word")

        def open_gate(c, a):
            nc.vector.tensor_copy(out=gate_word[:], in_=rotated(c, a)[:, 0, 0, 0:1])

        def store(c, a, h0=0, h1=GROUP_HEADS):
            nc.sync.dma_start(
                out=out_view[:, a, c * GROUP_COLS + h0 * HEAD : c * GROUP_COLS + h1 * HEAD],
                in_=result[(c, a)][:, h0:h1].rearrange("p h d -> p (h d)"),
            )

        LAST = GROUPS - 1
        EARLY_NOPE = 2
        prepare = {}
        for s in range(GROUPS * PASSES):
            prepare[s] = [("rope", s // PASSES, s % PASSES)]
            if s // PASSES < LAST:
                prepare[s].append(("nope", s // PASSES, s % PASSES))
        for g in range(EARLY_NOPE):
            prepare[LAST * PASSES + g].append(("nope", LAST, g))

        def scalar_share(s):
            for part, c, g in prepare.get(s, []):
                if part == "rope":
                    interleave("scalar", part, c, g, 0, SCALAR_HEADS.get(s, GROUP_HEADS), 0, ROPE)
                elif s in SCALAR_NOPE:
                    interleave("scalar", part, c, g, 0, GROUP_HEADS, SCALAR_NOPE[s], NOPE)

        def vector_share(s):
            if FIRST_SPLIT and s == 0:
                interleave("vector", "nope", 0, 0, 0, 2, 0, NOPE)
                interleave("vector", "rope", 0, 0, 2, 4, 0, ROPE)
                interleave("vector", "nope", 0, 0, 2, 4, 0, NOPE)
                return
            for part, c, g in prepare.get(s, []):
                if part == "nope":
                    if s < WEAVE_FROM and SCALAR_NOPE.get(s, NOPE) > 0:
                        interleave("vector", part, c, g, 0, GROUP_HEADS, 0, SCALAR_NOPE.get(s, NOPE))
                elif SCALAR_HEADS.get(s, GROUP_HEADS) < GROUP_HEADS:
                    interleave("vector", part, c, g, SCALAR_HEADS[s], GROUP_HEADS, 0, ROPE)

        def rotation(s):
            return s // PASSES - 1, s % PASSES

        def rotate(s):
            if s > PASSES:
                if s < GROUPS * PASSES:
                    open_gate(rotation(s - 1)[0], rotation(s - 1)[1])
                add_products(rotation(s - 1)[0], rotation(s - 1)[1])
            if not (SPLIT_LAST and s == STEPS - 1):
                first_product(rotation(s)[0], rotation(s)[1])
                second_product(rotation(s)[0], rotation(s)[1])
            if s > PASSES:
                if rotation(s - 1)[0] < LAST:
                    copy_unchanged("scalar", rotation(s - 1)[0], rotation(s - 1)[1])
                    store(rotation(s - 1)[0], rotation(s - 1)[1])

        scalar_share(0)
        for s in range(STEPS):
            for kind, lc, lg in loads[BLOCKS_AHEAD + s : BLOCKS_AHEAD + s + 1]:
                load(kind, lc, lg)
            if COPY_AT == 0 and (s == STEPS - 2 or s == STEPS - 1):
                for a in range(PASSES // 2):
                    copy_unchanged("scalar", LAST, (s - STEPS + 2) * 2 + a)
            if COPY_AT and s == STEPS - 1:
                for a in range(PASSES):
                    copy_unchanged("scalar", LAST, a)
            scalar_share(s + 1)
            if s == STEPS - PASSES - 1:
                for g in range(EARLY_NOPE, PASSES):
                    if not DEFER_WEAVE:
                        interleave("scalar", "nope", LAST, g, 0, GROUP_HEADS, 0, NOPE)
            if TABLES_AFTER and s == TABLES_STEP:
                make_tables()
            if EARLY_ROTATIONS and PASSES <= s < 2 * PASSES:
                rotate(s)
            if HIDDEN_FIRST and s in HIDDEN_STEP:
                quantize_hidden(HIDDEN_STEP.index(s))
            vector_share(s)
            if not HIDDEN_FIRST and s in HIDDEN_STEP:
                quantize_hidden(HIDDEN_STEP.index(s))
            for part, c, g in prepare.get(s, []):
                quantize(part, c, g)
            if s >= (2 * PASSES if EARLY_ROTATIONS else PASSES):
                rotate(s)
            for part, c, g in prepare.get(s + 1, []):
                if part == "nope" and s + 1 >= WEAVE_FROM:
                    copy_woven("vector", c, g)
            if s == STEPS - PASSES and not SPREAD:
                for g in range(EARLY_NOPE, PASSES):
                    quantize("nope", LAST, g)
            if SPREAD and STEPS - PASSES <= s < STEPS - EARLY_NOPE:
                quantize("nope", LAST, EARLY_NOPE + s - STEPS + PASSES)
            if COPY_AT == 0 and s == STEPS - 2:
                store(LAST, 0)
                store(LAST, 1)
            if COPY_AT and s == STEPS - 1:
                store(LAST, 0)
                store(LAST, 1)
            if s == STEPS - 1:
                store(LAST, 2)
            if PASSES - 1 <= s < STEPS - PASSES - 1:
                multiply("rope", rotation(s + 1)[0], rotation(s + 1)[1])
                if rotation(s + 1)[1] % 2 == 1:
                    multiply("nope", rotation(s + 1)[0], rotation(s + 1)[1] - 1)
                    multiply("nope", rotation(s + 1)[0], rotation(s + 1)[1])
            if s == STEPS - PASSES - 2:
                for a in range(TOKEN_TILES - 1):
                    multiply("rope", LAST, a, 0, PASSES - 1)
            if s == STEPS - PASSES - 1:
                for a in range(TOKEN_TILES - 1):
                    multiply("rope", LAST, a, PASSES - 1, PASSES)
                multiply("rope", LAST, TOKEN_TILES - 1)
                for g in range(EARLY_NOPE, PASSES):
                    if DEFER_WEAVE:
                        weave(LAST, g)
                        copy_woven("scalar", LAST, g)
            if PROGRESSIVE and STEPS - PASSES <= s < STEPS - EARLY_NOPE:
                g = EARLY_NOPE + s - STEPS + PASSES
                for a in range(TOKEN_TILES):
                    multiply("nope", LAST, a, 0 if g == EARLY_NOPE else g, g + 1)
            if not PROGRESSIVE and s == STEPS - PASSES + (1 if SPREAD else 0):
                for a in range(TOKEN_TILES):
                    multiply("nope", LAST, a)
            if s + 2 in HIDDEN_STEP:
                flip_hidden(HIDDEN_STEP.index(s + 2))
            for part, c, g in prepare.get(s + 2, []):
                if part == "nope" and s + 2 >= WEAVE_FROM:
                    weave(c, g)
        if SPLIT_LAST:
            for h0 in (0, 2):
                first_product(LAST, PASSES - 1, h0, h0 + 2)
                second_product(LAST, PASSES - 1, h0, h0 + 2)
            for h0 in (0, 2):
                add_products(LAST, PASSES - 1, h0, h0 + 2)
                store(LAST, PASSES - 1, h0, h0 + 2)
        else:
            add_products(LAST, PASSES - 1)
            store(LAST, PASSES - 1)
